import numpy as np
import ml_dtypes


def mxq(x, axis, fmt="e4m3"):
    dtype, down = {"e4m3": (ml_dtypes.float8_e4m3fn, 7), "e5m2": (ml_dtypes.float8_e5m2, 14)}[fmt]
    v = np.moveaxis(np.asarray(x, np.float32).astype(ml_dtypes.bfloat16).astype(np.float64), axis, -1)
    blocks = v.reshape(v.shape[:-1] + (-1, 32))
    amax = np.abs(blocks).max(-1, keepdims=True)
    byte = np.maximum(np.where(amax > 0, np.frexp(amax)[1] - 1 + 127, 0) - down, 1)
    scale = np.exp2(byte - 127.0)
    codes = (blocks / scale).astype(np.float32).astype(dtype).astype(np.float64)
    return np.moveaxis((codes * scale).reshape(v.shape), -1, axis)


WIDE = False


def mx_kscale(k):
    if not WIDE:
        return np.ones(k)
    levels = np.array([10, -10, 5, -5, 0])
    if k % 512:
        return np.exp2(np.random.permutation(np.resize(levels, k // 32))).repeat(32)
    a = np.empty((k // 512, 16))
    for p in range(k // 512):
        a[p, :8] = np.random.permutation(np.resize(levels, 8))
        for g in range(8):
            far = levels[np.abs(levels - a[p, g]) >= 10]
            a[p, g + 8] = far[np.random.randint(len(far))]
    return np.exp2(a.ravel()).repeat(32)


BF16 = ml_dtypes.bfloat16


def bf(x):
    return np.asarray(x, np.float32).astype(BF16)


def f64(x):
    return np.asarray(x).astype(np.float64)


B, S, D, H, DH, L, R = 1, 512, 2048, 16, 128, 1024, 64
DQK = L // 2
C = DH - R
HALF = R // 2


def rope(t):
    inv_freq = 1.0 / (10000.0 ** (np.arange(0, R, 2) / R))
    ang = np.arange(S)[:, None] * inv_freq[None, :]
    cos = np.cos(ang)[None, :, None, :]
    sin = np.sin(ang)[None, :, None, :]
    t1, t2 = t[..., :HALF], t[..., HALF:]
    return np.concatenate([t1 * cos - t2 * sin, t1 * sin + t2 * cos], axis=-1)


def draw0():
    s, t = mx_kscale(D), mx_kscale(DQK)
    return {"x": bf(np.random.standard_normal((B, S, D)) * s),
            "W_comp_qk": bf(np.random.standard_normal((D, DQK)) / np.sqrt(D) / s[:, None] * t),
            "W_q_dec": bf(np.random.standard_normal((DQK, H * C)) / np.sqrt(DQK) / t[:, None]),
            "W_k_dec": bf(np.random.standard_normal((DQK, H * C)) / np.sqrt(DQK) / t[:, None]),
            "W_rope_q": bf(np.random.standard_normal((D, H * R)) / np.sqrt(D) / s[:, None]),
            "W_rope_k": bf(np.random.standard_normal((D, H * R)) / np.sqrt(D) / s[:, None])}


def core(x, W_comp_qk, W_q_dec, W_k_dec, W_rope_q, W_rope_k):
    xq = mxq(f64(x), 2, "e4m3")
    c_qk = xq @ mxq(f64(W_comp_qk), 0, "e4m3")
    cq = mxq(c_qk, 2, "e4m3")
    q_no_rope = cq @ mxq(f64(W_q_dec), 0, "e4m3")
    k_no_rope = cq @ mxq(f64(W_k_dec), 0, "e4m3")
    q_rope = xq @ mxq(f64(W_rope_q), 0, "e4m3")
    k_rope = xq @ mxq(f64(W_rope_k), 0, "e4m3")
    q = np.concatenate([q_no_rope, q_rope], axis=-1).reshape(B, S, H, DH)
    k = np.concatenate([k_no_rope, k_rope], axis=-1).reshape(B, S, H, DH)
    q = np.concatenate([q[..., :C], rope(q[..., C:])], axis=-1)
    k = np.concatenate([k[..., :C], rope(k[..., C:])], axis=-1)
    return q, k


def e4m3fn_bytes(y):
    return np.clip(np.asarray(y, np.float64), -448.0, 448.0).astype(np.float32).astype(ml_dtypes.float8_e4m3fn).view(np.uint8)


def e4m3fn_values(b):
    return np.asarray(b, np.uint8).view(ml_dtypes.float8_e4m3fn).astype(np.float64)


def setup_inputs():
    d = draw0()
    x0 = np.asarray(d['W_rope_q']).astype(np.float64)
    s = (np.max(np.abs(x0), axis=(1,), keepdims=True) / 448.0).astype(np.float32)
    out = {}
    for k, v in d.items():
        if k == 'W_rope_q':
            out['W_rope_q_bytes'] = e4m3fn_bytes(x0 / s.astype(np.float64))
            out['W_rope_q_scale'] = s
        else:
            out[k] = v
    return out


def reference(x, W_comp_qk, W_q_dec, W_k_dec, W_rope_q_bytes, W_rope_q_scale, W_rope_k):
    return core(x, W_comp_qk, W_q_dec, W_k_dec, e4m3fn_values(W_rope_q_bytes) * W_rope_q_scale.astype(np.float64), W_rope_k)

@@ -1,0 +1,306 @@
+import math
+from contextlib import ExitStack
+
+import concourse.mybir as mybir
+from concourse.masks import make_identity
+
+F32 = mybir.dt.float32
+BF16 = mybir.dt.bfloat16
+I32 = mybir.dt.int32
+U32 = mybir.dt.uint32
+U8 = mybir.dt.uint8
+FP8 = mybir.dt.float8_e4m3fn
+FP8X4 = mybir.dt.float8_e4m3fn_x4
+ALU = mybir.AluOpType
+ACT = mybir.ActivationFunctionType
+
+P = 128
+S, D, H, DH, LQK, R = 512, 2048, 16, 128, 512, 64
+C = DH - R
+HALF = R // 2
+TT = S // P
+NG = D // 512
+FLOPS = 2 * (S * D * LQK + 2 * S * LQK * H * C + 2 * S * D * H * R)
+
+V_C = 512
+V_DEC = 320
+V_RQ = 224
+V_RK = 176
+
+
+def tile_multiheadlatentattention_pa_kernel(
+    tc, x, w_c, w_qd, w_kd, w_rq_bytes, w_rq_scale, w_rk, out_q, out_k
+):
+    nc = tc.nc
+    with ExitStack() as ctx:
+        keep = ctx.enter_context(tc.tile_pool(name="keep", bufs=1))
+        work = ctx.enter_context(tc.tile_pool(name="work", bufs=3))
+        psum = ctx.enter_context(tc.psum_pool(name="psum", bufs=8))
+
+        warm = keep.tile([P, 1], F32, name="warm")
+        nc.gpsimd.memset(warm[:], 0.0)
+        warm2 = keep.tile([P, 1], F32, name="warm2")
+        nc.scalar.activation(out=warm2[:], in_=warm[:], func=ACT.Sin)
+        ident = keep.tile([P, P], F32, name="ident")
+        make_identity(nc, ident[:])
+
+        x_raw = [keep.tile([P, D], BF16, name="x_raw%d" % t) for t in range(TT)]
+        c_raw = [keep.tile([P, 4, 512], BF16, name="c_raw%d" % g) for g in range(NG)]
+        qb_raw = [keep.tile([P, 4, 1024], U8, name="qb_raw%d" % g) for g in range(NG)]
+        k_raw = [keep.tile([P, 4, 1024], BF16, name="k_raw%d" % g) for g in range(NG)]
+        qd_raw = keep.tile([P, 4, 1024], BF16, name="qd_raw")
+        kd_raw = keep.tile([P, 4, 1024], BF16, name="kd_raw")
+        q_scale = keep.tile([P, NG, 4], F32, name="q_scale")
+
+        x_rows = x.rearrange("b s d -> (b s) d")
+
+        def load_x(t):
+            nc.sync.dma_start(out=x_raw[t][:], in_=x_rows[t * P : (t + 1) * P, :])
+
+        def load_w(tiles, src, g):
+            nc.sync.dma_start(
+                out=tiles[g][:], in_=src[g * 512 : (g + 1) * 512, :].rearrange("(p t) n -> p t n", t=4)
+            )
+
+        nc.scalar.dma_start(
+            out=q_scale[:], in_=w_rq_scale.rearrange("(g p t) o -> p g (t o)", p=P, t=4)
+        )
+        load_w(qb_raw, w_rq_bytes, 0)
+        for i in range(4):
+            load_w(c_raw, w_c, i)
+            load_x(i)
+        load_w([qd_raw], w_qd, 0)
+        load_w(qb_raw, w_rq_bytes, 1)
+        load_w(qb_raw, w_rq_bytes, 2)
+        load_w(qb_raw, w_rq_bytes, 3)
+        load_w([kd_raw], w_kd, 0)
+        for g in range(NG):
+            load_w(k_raw, w_rk, g)
+
+        pos = keep.tile([P, TT, 1], F32, name="pos")
+        nc.gpsimd.iota(
+            pos[:], pattern=[[P, TT], [0, 1]], base=0, channel_multiplier=1, allow_small_or_imprecise_dtypes=True
+        )
+        turns = keep.tile([P, TT, HALF], F32, name="turns")
+        for i in range(HALF):
+            nc.gpsimd.tensor_scalar(
+                out=turns[:, :, i : i + 1],
+                in0=pos[:],
+                scalar1=1.0 / (10000.0 ** (2.0 * i / R)) / (2.0 * math.pi),
+                scalar2=None,
+                op0=ALU.mult,
+            )
+        table = keep.tile([P, TT, 2, 2, HALF], F32, name="table")
+
+        def operand(name, parts, width):
+            codes = keep.tile([P, parts, width], U32, name=name + "_codes", align_bytes=64)
+            scales = keep.tile([P, parts, width], U8, name=name + "_scales", align_bytes=64)
+            return codes, scales
+
+        x_op = operand("x", TT * NG, P)
+        c_w_op = operand("c_w", NG, 512)
+        c_op = operand("c", TT, P)
+        qd_op = operand("qd", 1, 1024)
+        kd_op = operand("kd", 1, 1024)
+        rq_op = operand("rq", NG, 1024)
+        rk_op = operand("rk", NG, 1024)
+
+        def quantize(op, part, cols, grouped):
+            nc.vector.quantize_mx(
+                out=op[0][:, part, cols].bitcast(FP8X4), scales=op[1][:, part, cols], in_=grouped
+            )
+
+        def x_step(t):
+            xg = work.tile([P, NG * P * 4], BF16, name="xg", tag="stage", bufs=6, align_bytes=64)
+            words = x_raw[t][:].bitcast(F32)
+            xw = xg[:].bitcast(F32).rearrange("p (g r u) -> p g r u", g=NG, u=2)
+            for b in range(2):
+                xt = psum.tile([P, 2, 2, P], F32, name="bank")
+                for e in range(2):
+                    g = 2 * b + e
+                    for u in range(2):
+                        nc.tensor.transpose(
+                            xt[:, e, u, :], words[:, 256 * g + u : 256 * (g + 1) : 2], ident[:]
+                        )
+                nc.scalar.copy(out=xw[:, 2 * b : 2 * b + 2], in_=xt[:].rearrange("p g u r -> p g r u"))
+            nc.vector.quantize_mx(
+                out=x_op[0][:, t * NG : (t + 1) * NG, :].rearrange("p g n -> p (g n)").bitcast(FP8X4),
+                scales=x_op[1][:, t * NG : (t + 1) * NG, :].rearrange("p g n -> p (g n)"),
+                in_=xg[:],
+            )
+
+        def interleave(raw, v_cols):
+            grouped = work.tile([P, 512, 4], BF16, name="grouped", tag="stage", bufs=6, align_bytes=64)
+            for eng, lo, hi in ((nc.vector.tensor_copy, 0, v_cols), (nc.scalar.copy, v_cols, 512)):
+                if hi > lo:
+                    eng(
+                        out=grouped[:, lo:hi, :].rearrange("p (c i) t -> p c t i", i=4),
+                        in_=raw[:, :, lo:hi].rearrange("p t (c i) -> p c t i", i=4),
+                    )
+            return grouped[:].rearrange("p n t -> p (n t)")
+
+        def cw_step(g):
+            grouped = work.tile([P, 512 * 4], BF16, name="cgrouped", tag="stage", bufs=6, align_bytes=64)
+            nc.vector.tensor_copy(
+                out=grouped[:].rearrange("p (t m j) -> p t m j", t=4, j=4),
+                in_=c_raw[g][:].rearrange("p j (m t) -> p t m j", t=4),
+            )
+            quantize(c_w_op, g, slice(0, 512), grouped[:])
+
+        def c_step(t):
+            cb = psum.tile([P, 4, P], F32, name="bank")
+            for j in range(4):
+                for g in range(NG):
+                    nc.tensor.matmul_mx(
+                        out=cb[:, j, :],
+                        lhsT=c_w_op[0][:, g, j * P : (j + 1) * P].bitcast(FP8X4),
+                        lhsT_scale=c_w_op[1][:, g, j * P : (j + 1) * P],
+                        rhs=x_op[0][:, t * NG + g, :].bitcast(FP8X4),
+                        rhs_scale=x_op[1][:, t * NG + g, :],
+                        start=(g == 0),
+                        stop=(g == NG - 1),
+                    )
+            cg = work.tile([P, P, 4], BF16, name="cg", bufs=2, align_bytes=64)
+            nc.scalar.copy(out=cg[:], in_=cb[:].rearrange("p t n -> p n t"))
+            quantize(c_op, t, slice(0, P), cg[:].rearrange("p n t -> p (n t)"))
+
+        def dec_prep(op, raw, half_no):
+            cols = slice(half_no * 512, half_no * 512 + 512)
+            quantize(op, 0, cols, interleave(raw[:, :, cols], V_DEC))
+
+        def rk_prep(g, half_no):
+            cols = slice(half_no * 512, half_no * 512 + 512)
+            quantize(rk_op, g, cols, interleave(k_raw[g][:, :, cols], V_RK))
+
+        def rq_prep(g, half_no):
+            cols = slice(half_no * 512, half_no * 512 + 512)
+            wide = work.tile([P, 4, 512], BF16, name="wide", bufs=3, align_bytes=64)
+            for j in range(4):
+                nc.scalar.activation(
+                    out=wide[:, j, :],
+                    in_=qb_raw[g][:, j, cols].bitcast(FP8),
+                    func=ACT.Copy,
+                    scale=q_scale[:, g, j : j + 1],
+                )
+            quantize(rq_op, g, cols, interleave(wide[:], V_RQ))
+
+        q_rows = out_q.rearrange("b s h d -> (b s) (h d)").rearrange("(t p) c -> p t c", p=P)
+        k_rows = out_k.rearrange("b s h d -> (b s) (h d)").rearrange("(t p) c -> p t c", p=P)
+
+        def finish(banks, rows, pair, col0):
+            res = work.tile([P, 2, 4, DH], F32, name="res", bufs=3)
+            prod = work.tile([P, 2, 2, 4, R], F32, name="prod", bufs=3)
+            for e in range(2):
+                acc = banks[e][:].rearrange("p (h d) -> p h d", h=4)
+                nc.vector.tensor_tensor(
+                    out=prod[:, :, e],
+                    in0=acc[:, :, C:DH].unsqueeze(1).to_broadcast([P, 2, 4, R]),
+                    in1=table[:, 2 * pair + e]
+                    .rearrange("p c j i -> p c (j i)")
+                    .unsqueeze(2)
+                    .to_broadcast([P, 2, 4, R]),
+                    op=ALU.mult,
+                )
+                nc.scalar.copy(out=res[:, e, :, 0:C], in_=acc[:, :, 0:C])
+            p1 = prod[:, 0].rearrange("p e h (j i) -> p (e h) j i", j=2)
+            p2 = prod[:, 1].rearrange("p e h (j i) -> p (e h) j i", j=2)
+            nc.vector.tensor_tensor(
+                out=res[:, :, :, C:DH].rearrange("p e h (j i) -> p (e h) j i", j=2),
+                in0=p1,
+                in1=p2[:, :, ::-1, :],
+                op=ALU.add,
+            )
+            nc.sync.dma_start(
+                out=rows[:, 2 * pair : 2 * pair + 2, col0 : col0 + 512],
+                in_=res[:].rearrange("p e h d -> p e (h d)"),
+            )
+
+        def dec_out(op, rows, half_no):
+            cols = slice(half_no * 512, half_no * 512 + 512)
+            for pair in range(2):
+                banks = []
+                for e in range(2):
+                    t = 2 * pair + e
+                    acc = psum.tile([P, 512], F32, name="bank")
+                    nc.tensor.matmul_mx(
+                        out=acc[:],
+                        lhsT=c_op[0][:, t, :].bitcast(FP8X4),
+                        lhsT_scale=c_op[1][:, t, :],
+                        rhs=op[0][:, 0, cols].bitcast(FP8X4),
+                        rhs_scale=op[1][:, 0, cols],
+                        start=True,
+                        stop=True,
+                    )
+                    banks.append(acc)
+                finish(banks, rows, pair, half_no * 512)
+
+        def rope_out(op, rows, half_no):
+            cols = slice(half_no * 512, half_no * 512 + 512)
+            banks = [psum.tile([P, 512], F32, name="bank") for t in range(TT)]
+            for g in range(NG):
+                for t in range(TT):
+                    nc.tensor.matmul_mx(
+                        out=banks[t][:],
+                        lhsT=x_op[0][:, t * NG + g, :].bitcast(FP8X4),
+                        lhsT_scale=x_op[1][:, t * NG + g, :],
+                        rhs=op[0][:, g, cols].bitcast(FP8X4),
+                        rhs_scale=op[1][:, g, cols],
+                        start=(g == 0),
+                        stop=(g == NG - 1),
+                    )
+            for pair in range(2):
+                finish(banks[2 * pair : 2 * pair + 2], rows, pair, 1024 + half_no * 512)
+
+        for i in range(4):
+            x_step(i)
+            cw_step(i)
+        rq_prep(0, 0)
+        whole = keep.tile([P, TT, HALF], I32, name="whole")
+        nc.vector.tensor_copy(out=whole[:], in_=turns[:])
+        frac = keep.tile([P, TT, HALF], F32, name="frac")
+        nc.vector.tensor_tensor(out=frac[:], in0=turns[:], in1=whole[:], op=ALU.subtract)
+        nfrac = keep.tile([P, TT, HALF], F32, name="nfrac")
+        nc.vector.scalar_tensor_tensor(
+            out=nfrac[:], in0=frac[:], scalar=0.5, in1=frac[:], op0=ALU.is_gt, op1=ALU.subtract
+        )
+        half = keep.tile([P, TT, HALF], F32, name="half")
+        half2 = keep.tile([P, TT, HALF], F32, name="half2")
+        nc.scalar.activation(out=half[:], in_=nfrac[:], func=ACT.Sin, scale=math.pi)
+        nc.scalar.activation(out=table[:, :, 1, 0, :], in_=nfrac[:], func=ACT.Sin, scale=-2.0 * math.pi)
+        nc.scalar.activation(out=table[:, :, 1, 1, :], in_=nfrac[:], func=ACT.Sin, scale=2.0 * math.pi)
+        nc.vector.scalar_tensor_tensor(
+            out=half2[:], in0=half[:], scalar=-2.0, in1=half[:], op0=ALU.mult, op1=ALU.mult
+        )
+        for j in range(2):
+            nc.vector.tensor_scalar(
+                out=table[:, :, 0, j, :], in0=half2[:], scalar1=1.0, scalar2=None, op0=ALU.add
+            )
+        for t in range(TT):
+            c_step(t)
+        dec_prep(qd_op, qd_raw, 0)
+        dec_prep(qd_op, qd_raw, 1)
+        rq_prep(1, 0)
+        dec_out(qd_op, q_rows, 0)
+        rq_prep(2, 0)
+        rq_prep(3, 0)
+        dec_out(qd_op, q_rows, 1)
+        rq_prep(0, 1)
+        rq_prep(1, 1)
+        rope_out(rq_op, q_rows, 0)
+        rq_prep(2, 1)
+        rq_prep(3, 1)
+        dec_prep(kd_op, kd_raw, 0)
+        dec_prep(kd_op, kd_raw, 1)
+        dec_out(kd_op, k_rows, 0)
+        rk_prep(0, 0)
+        rk_prep(1, 0)
+        rope_out(rq_op, q_rows, 1)
+        rk_prep(2, 0)
+        rk_prep(3, 0)
+        dec_out(kd_op, k_rows, 1)
+        rk_prep(0, 1)
+        rk_prep(1, 1)
+        rope_out(rk_op, k_rows, 0)
+        rk_prep(2, 1)
+        rk_prep(3, 1)
+        rope_out(rk_op, k_rows, 1)

@@ -22,10 +22,8 @@ TT = S // P
 NG = D // 512
 FLOPS = 2 * (S * D * LQK + 2 * S * LQK * H * C + 2 * S * D * H * R)
 
-V_C = 512
-V_DEC = 320
-V_RQ = 224
-V_RK = 176
+V_COLS = [320,320,0,0,0,0,256,256,0,0,0,0,96,96,96,96,96,96,256,256]
+V_PLANES = [1,2,2,2]
 
 
 def tile_multiheadlatentattention_pa_kernel(
@@ -43,11 +41,12 @@ def tile_multiheadlatentattention_pa_kernel(
         nc.scalar.activation(out=warm2[:], in_=warm[:], func=ACT.Sin)
         ident = keep.tile([P, P], F32, name="ident")
         make_identity(nc, ident[:])
+        ident_b = keep.tile([P, P], BF16, name="ident_b")
+        make_identity(nc, ident_b[:])
 
-        x_raw = [keep.tile([P, D], BF16, name="x_raw%d" % t) for t in range(TT)]
-        c_raw = [keep.tile([P, 4, 512], BF16, name="c_raw%d" % g) for g in range(NG)]
+        x_pair = [keep.tile([P, 2, D], BF16, name="x_pair%d" % t, tag="big", bufs=4) for t in range(2)]
+        c_pair = [keep.tile([P, 2, 4, 512], BF16, name="c_pair%d" % t, tag="big", bufs=4) for t in range(2)]
         qb_raw = [keep.tile([P, 4, 1024], U8, name="qb_raw%d" % g) for g in range(NG)]
-        k_raw = [keep.tile([P, 4, 1024], BF16, name="k_raw%d" % g) for g in range(NG)]
         qd_raw = keep.tile([P, 4, 1024], BF16, name="qd_raw")
         kd_raw = keep.tile([P, 4, 1024], BF16, name="kd_raw")
         q_scale = keep.tile([P, NG, 4], F32, name="q_scale")
@@ -55,27 +54,25 @@ def tile_multiheadlatentattention_pa_kernel(
         x_rows = x.rearrange("b s d -> (b s) d")
 
         def load_x(t):
-            nc.sync.dma_start(out=x_raw[t][:], in_=x_rows[t * P : (t + 1) * P, :])
+            nc.sync.dma_start(out=x_pair[t // 2][:, t % 2], in_=x_rows[t * P : (t + 1) * P, :])
 
-        def load_w(tiles, src, g):
+        def load_w(dst, src, g):
             nc.sync.dma_start(
-                out=tiles[g][:], in_=src[g * 512 : (g + 1) * 512, :].rearrange("(p t) n -> p t n", t=4)
+                out=dst, in_=src[g * 512 : (g + 1) * 512, :].rearrange("(p t) n -> p t n", t=4)
             )
 
         nc.scalar.dma_start(
             out=q_scale[:], in_=w_rq_scale.rearrange("(g p t) o -> p g (t o)", p=P, t=4)
         )
-        load_w(qb_raw, w_rq_bytes, 0)
+        load_w(qb_raw[0][:], w_rq_bytes, 0)
         for i in range(4):
-            load_w(c_raw, w_c, i)
+            load_w(c_pair[i // 2][:, i % 2], w_c, i)
             load_x(i)
-        load_w([qd_raw], w_qd, 0)
-        load_w(qb_raw, w_rq_bytes, 1)
-        load_w(qb_raw, w_rq_bytes, 2)
-        load_w(qb_raw, w_rq_bytes, 3)
-        load_w([kd_raw], w_kd, 0)
-        for g in range(NG):
-            load_w(k_raw, w_rk, g)
+        load_w(qd_raw[:], w_qd, 0)
+        load_w(qb_raw[1][:], w_rq_bytes, 1)
+        load_w(kd_raw[:], w_kd, 0)
+        load_w(qb_raw[2][:], w_rq_bytes, 2)
+        load_w(qb_raw[3][:], w_rq_bytes, 3)
 
         pos = keep.tile([P, TT, 1], F32, name="pos")
         nc.gpsimd.iota(
@@ -110,9 +107,11 @@ def tile_multiheadlatentattention_pa_kernel(
                 out=op[0][:, part, cols].bitcast(FP8X4), scales=op[1][:, part, cols], in_=grouped
             )
 
-        def x_step(t):
+        xgs = {}
+
+        def x_turn(t):
             xg = work.tile([P, NG * P * 4], BF16, name="xg", tag="stage", bufs=6, align_bytes=64)
-            words = x_raw[t][:].bitcast(F32)
+            words = x_pair[t // 2][:, t % 2].bitcast(F32)
             xw = xg[:].bitcast(F32).rearrange("p (g r u) -> p g r u", g=NG, u=2)
             for b in range(2):
                 xt = psum.tile([P, 2, 2, P], F32, name="bank")
@@ -123,31 +122,31 @@ def tile_multiheadlatentattention_pa_kernel(
                             xt[:, e, u, :], words[:, 256 * g + u : 256 * (g + 1) : 2], ident[:]
                         )
                 nc.scalar.copy(out=xw[:, 2 * b : 2 * b + 2], in_=xt[:].rearrange("p g u r -> p g r u"))
+            xgs[t] = xg
+
+        def x_quant(t):
             nc.vector.quantize_mx(
                 out=x_op[0][:, t * NG : (t + 1) * NG, :].rearrange("p g n -> p (g n)").bitcast(FP8X4),
                 scales=x_op[1][:, t * NG : (t + 1) * NG, :].rearrange("p g n -> p (g n)"),
-                in_=xg[:],
+                in_=xgs[t][:],
             )
 
-        def interleave(raw, v_cols):
-            grouped = work.tile([P, 512, 4], BF16, name="grouped", tag="stage", bufs=6, align_bytes=64)
-            for eng, lo, hi in ((nc.vector.tensor_copy, 0, v_cols), (nc.scalar.copy, v_cols, 512)):
-                if hi > lo:
-                    eng(
-                        out=grouped[:, lo:hi, :].rearrange("p (c i) t -> p c t i", i=4),
-                        in_=raw[:, :, lo:hi].rearrange("p t (c i) -> p c t i", i=4),
-                    )
-            return grouped[:].rearrange("p n t -> p (n t)")
+        cgs = {}
 
-        def cw_step(g):
+        def cw_turn(g):
             grouped = work.tile([P, 512 * 4], BF16, name="cgrouped", tag="stage", bufs=6, align_bytes=64)
             nc.vector.tensor_copy(
                 out=grouped[:].rearrange("p (t m j) -> p t m j", t=4, j=4),
-                in_=c_raw[g][:].rearrange("p j (m t) -> p t m j", t=4),
+                in_=c_pair[g // 2][:, g % 2].rearrange("p j (m t) -> p t m j", t=4),
             )
-            quantize(c_w_op, g, slice(0, 512), grouped[:])
+            cgs[g] = grouped
 
-        def c_step(t):
+        def cw_quant(g):
+            quantize(c_w_op, g, slice(0, 512), cgs[g][:])
+
+        lat = {}
+
+        def c_mm(t):
             cb = psum.tile([P, 4, P], F32, name="bank")
             for j in range(4):
                 for g in range(NG):
@@ -162,145 +161,240 @@ def tile_multiheadlatentattention_pa_kernel(
                     )
             cg = work.tile([P, P, 4], BF16, name="cg", bufs=2, align_bytes=64)
             nc.scalar.copy(out=cg[:], in_=cb[:].rearrange("p t n -> p n t"))
-            quantize(c_op, t, slice(0, P), cg[:].rearrange("p n t -> p (n t)"))
+            lat[t] = cg
 
-        def dec_prep(op, raw, half_no):
-            cols = slice(half_no * 512, half_no * 512 + 512)
-            quantize(op, 0, cols, interleave(raw[:, :, cols], V_DEC))
+        def c_quant(t):
+            quantize(c_op, t, slice(0, P), lat[t][:].rearrange("p n t -> p (n t)"))
 
-        def rk_prep(g, half_no):
-            cols = slice(half_no * 512, half_no * 512 + 512)
-            quantize(rk_op, g, cols, interleave(k_raw[g][:, :, cols], V_RK))
+        def cols_of(half_no):
+            return slice(half_no * 512, half_no * 512 + 512)
 
-        def rq_prep(g, half_no):
-            cols = slice(half_no * 512, half_no * 512 + 512)
-            wide = work.tile([P, 4, 512], BF16, name="wide", bufs=3, align_bytes=64)
-            for j in range(4):
-                nc.scalar.activation(
-                    out=wide[:, j, :],
-                    in_=qb_raw[g][:, j, cols].bitcast(FP8),
-                    func=ACT.Copy,
-                    scale=q_scale[:, g, j : j + 1],
-                )
-            quantize(rq_op, g, cols, interleave(wide[:], V_RQ))
+        wides = {}
+        groups = {}
+
+        def widen(g, planes):
+            if g not in wides:
+                wide = work.tile([P, 4, 1024], BF16, name="wide", bufs=2, align_bytes=64)
+                wides[g] = wide
+            for j in planes:
+                src = qb_raw[g][:, j, :].bitcast(FP8)
+                if j < V_PLANES[g]:
+                    nc.vector.tensor_scalar(
+                        out=wides[g][:, j, :], in0=src, scalar1=q_scale[:, g, j : j + 1], scalar2=None, op0=ALU.mult
+                    )
+                else:
+                    nc.scalar.activation(
+                        out=wides[g][:, j, :], in_=src, func=ACT.Copy, scale=q_scale[:, g, j : j + 1]
+                    )
+
+        def source(unit):
+            kind, half_no, g = unit
+            if kind == "rq":
+                return wides[g][:, :, cols_of(half_no)]
+            if kind == "rk":
+                return k_raw[g][:, :, cols_of(half_no)]
+            return {"qd": qd_raw, "kd": kd_raw}[kind][:, :, cols_of(half_no)]
+
+        def turn(unit, v_cols):
+            raw = source(unit)
+            grouped = work.tile([P, 512, 4], BF16, name="grouped", tag="stage", bufs=6, align_bytes=64)
+            groups[unit] = grouped
+            if unit[0] == "rq":
+                for b in range(2):
+                    pb = psum.tile([P, 2, 512], BF16, name="pbank", tag="bank")
+                    for e in range(2):
+                        n0 = b * 256 + e * P
+                        nc.tensor.matmul(
+                            out=pb[:, e, :].rearrange("p (n t) -> p n t", t=4),
+                            lhsT=ident_b[:],
+                            rhs=raw[:, :, n0 : n0 + P].rearrange("p t n -> p n t"),
+                            start=True,
+                            stop=True,
+                        )
+                    nc.scalar.copy(
+                        out=grouped[:, b * 256 : b * 256 + 256, :].rearrange("p n t -> p (n t)"),
+                        in_=pb[:].rearrange("p e c -> p (e c)"),
+                    )
+                return
+            for eng, lo, hi in ((nc.vector.tensor_copy, 0, v_cols), (nc.scalar.copy, v_cols, 512)):
+                if hi > lo:
+                    eng(
+                        out=grouped[:, lo:hi, :].rearrange("p (c i) t -> p c t i", i=4),
+                        in_=raw[:, :, lo:hi].rearrange("p t (c i) -> p c t i", i=4),
+                    )
+
+        ops = {"qd": qd_op, "kd": kd_op, "rq": rq_op, "rk": rk_op}
+
+        def unit_quant(unit):
+            kind, half_no, g = unit
+            quantize(ops[kind], g, cols_of(half_no), groups[unit][:].rearrange("p n t -> p (n t)"))
 
         q_rows = out_q.rearrange("b s h d -> (b s) (h d)").rearrange("(t p) c -> p t c", p=P)
         k_rows = out_k.rearrange("b s h d -> (b s) (h d)").rearrange("(t p) c -> p t c", p=P)
+        rows_of = {"qd": q_rows, "kd": k_rows, "rq": q_rows, "rk": k_rows}
+        accs = {}
+        prods = {}
+        ress = {}
 
-        def finish(banks, rows, pair, col0):
-            res = work.tile([P, 2, 4, DH], F32, name="res", bufs=3)
-            prod = work.tile([P, 2, 2, 4, R], F32, name="prod", bufs=3)
+        def mm(kind, half_no, t, g):
+            op = ops[kind]
+            cols = cols_of(half_no)
+            last = 0 if kind in ("qd", "kd") else NG - 1
+            if g == 0:
+                acc = psum.tile([P, 512], F32, name="bank")
+                accs[(kind, half_no, t)] = acc
+            src, part = (c_op, t) if last == 0 else (x_op, t * NG + g)
+            nc.tensor.matmul_mx(
+                out=accs[(kind, half_no, t)][:],
+                lhsT=src[0][:, part, :].bitcast(FP8X4),
+                lhsT_scale=src[1][:, part, :],
+                rhs=op[0][:, g, cols].bitcast(FP8X4),
+                rhs_scale=op[1][:, g, cols],
+                start=(g == 0),
+                stop=(g == last),
+            )
+
+        def mm_pair(out):
+            kind, half_no, pair = out
             for e in range(2):
-                acc = banks[e][:].rearrange("p (h d) -> p h d", h=4)
-                nc.vector.tensor_tensor(
-                    out=prod[:, :, e],
-                    in0=acc[:, :, C:DH].unsqueeze(1).to_broadcast([P, 2, 4, R]),
-                    in1=table[:, 2 * pair + e]
-                    .rearrange("p c j i -> p c (j i)")
-                    .unsqueeze(2)
-                    .to_broadcast([P, 2, 4, R]),
-                    op=ALU.mult,
-                )
-                nc.scalar.copy(out=res[:, e, :, 0:C], in_=acc[:, :, 0:C])
-            p1 = prod[:, 0].rearrange("p e h (j i) -> p (e h) j i", j=2)
+                for g in range(1 if kind in ("qd", "kd") else NG):
+                    mm(kind, half_no, 2 * pair + e, g)
+
+        def heads(out, e):
+            kind, half_no, pair = out
+            return accs[(kind, half_no, 2 * pair + e)][:].rearrange("p (h d) -> p h d", h=4)
+
+        def products(out, e):
+            if e == 0:
+                prod = work.tile([P, 2, 2, 4, R], F32, name="prod", bufs=3)
+                prods[out] = prod
+            nc.vector.tensor_tensor(
+                out=prods[out][:, :, e],
+                in0=heads(out, e)[:, :, C:DH].unsqueeze(1).to_broadcast([P, 2, 4, R]),
+                in1=table[:, 2 * out[2] + e]
+                .rearrange("p c j i -> p c (j i)")
+                .unsqueeze(2)
+                .to_broadcast([P, 2, 4, R]),
+                op=ALU.mult,
+            )
+
+        def plain(out, e):
+            if e == 0:
+                res = work.tile([P, 2, 4, DH], F32, name="res", bufs=5)
+                ress[out] = res
+            nc.scalar.copy(out=ress[out][:, e, :, 0:C], in_=heads(out, e)[:, :, 0:C])
+
+        def add_store(out):
+            kind, half_no, pair = out
+            prod = prods[out]
+            res = ress[out]
             p2 = prod[:, 1].rearrange("p e h (j i) -> p (e h) j i", j=2)
             nc.vector.tensor_tensor(
                 out=res[:, :, :, C:DH].rearrange("p e h (j i) -> p (e h) j i", j=2),
-                in0=p1,
+                in0=prod[:, 0].rearrange("p e h (j i) -> p (e h) j i", j=2),
                 in1=p2[:, :, ::-1, :],
                 op=ALU.add,
             )
+            col0 = half_no * 512 + (0 if kind in ("qd", "kd") else 1024)
             nc.sync.dma_start(
-                out=rows[:, 2 * pair : 2 * pair + 2, col0 : col0 + 512],
+                out=rows_of[kind][:, 2 * pair : 2 * pair + 2, col0 : col0 + 512],
                 in_=res[:].rearrange("p e h d -> p e (h d)"),
             )
 
-        def dec_out(op, rows, half_no):
-            cols = slice(half_no * 512, half_no * 512 + 512)
-            for pair in range(2):
-                banks = []
-                for e in range(2):
-                    t = 2 * pair + e
-                    acc = psum.tile([P, 512], F32, name="bank")
-                    nc.tensor.matmul_mx(
-                        out=acc[:],
-                        lhsT=c_op[0][:, t, :].bitcast(FP8X4),
-                        lhsT_scale=c_op[1][:, t, :],
-                        rhs=op[0][:, 0, cols].bitcast(FP8X4),
-                        rhs_scale=op[1][:, 0, cols],
-                        start=True,
-                        stop=True,
-                    )
-                    banks.append(acc)
-                finish(banks, rows, pair, half_no * 512)
+        units = [("qd", 0, 0), ("qd", 1, 0)]
+        units += [("rq", half_no, g) for g in range(2) for half_no in range(2)]
+        units += [("kd", 0, 0), ("kd", 1, 0)]
+        units += [("rq", half_no, g) for g in range(2, 4) for half_no in range(2)]
+        units += [("rk", half_no, g) for half_no in range(2) for g in range(NG)]
+        n = len(units)
+        outs = {}
+        for s, out in enumerate([("qd", h, p) for h in range(2) for p in range(2)]):
+            outs[2 + s] = out
+        for s, out in enumerate([("kd", h, p) for h in range(2) for p in range(2)]):
+            outs[8 + s] = out
+        for s, out in enumerate([("rq", h, p) for h in range(2) for p in range(2)]):
+            outs[12 + s] = out
+        for s, out in enumerate([("rk", 0, p) for p in range(2)]):
+            outs[16 + s] = out
+        widen_at = {0: (1, (0, 1)), 1: (1, (2, 3)), 4: (2, (0, 1)), 5: (2, (2, 3)), 6: (3, (0, 1)), 7: (3, (2, 3))}
 
-        def rope_out(op, rows, half_no):
-            cols = slice(half_no * 512, half_no * 512 + 512)
-            banks = [psum.tile([P, 512], F32, name="bank") for t in range(TT)]
+        with tc.manual_schedule():
+            widen(0, (0, 1))
+            for i in range(4):
+                cw_turn(i)
+                x_turn(i)
+                if i == 0:
+                    widen(0, (2, 3))
+                if i > 0:
+                    cw_quant(i - 1)
+                    x_quant(i - 1)
+            turn(units[0], V_COLS[0])
+            cw_quant(3)
+            x_quant(3)
+            k_raw = []
             for g in range(NG):
-                for t in range(TT):
-                    nc.tensor.matmul_mx(
-                        out=banks[t][:],
-                        lhsT=x_op[0][:, t * NG + g, :].bitcast(FP8X4),
-                        lhsT_scale=x_op[1][:, t * NG + g, :],
-                        rhs=op[0][:, g, cols].bitcast(FP8X4),
-                        rhs_scale=op[1][:, g, cols],
-                        start=(g == 0),
-                        stop=(g == NG - 1),
-                    )
-            for pair in range(2):
-                finish(banks[2 * pair : 2 * pair + 2], rows, pair, 1024 + half_no * 512)
-
-        for i in range(4):
-            x_step(i)
-            cw_step(i)
-        rq_prep(0, 0)
-        whole = keep.tile([P, TT, HALF], I32, name="whole")
-        nc.vector.tensor_copy(out=whole[:], in_=turns[:])
-        frac = keep.tile([P, TT, HALF], F32, name="frac")
-        nc.vector.tensor_tensor(out=frac[:], in0=turns[:], in1=whole[:], op=ALU.subtract)
-        nfrac = keep.tile([P, TT, HALF], F32, name="nfrac")
-        nc.vector.scalar_tensor_tensor(
-            out=nfrac[:], in0=frac[:], scalar=0.5, in1=frac[:], op0=ALU.is_gt, op1=ALU.subtract
-        )
-        half = keep.tile([P, TT, HALF], F32, name="half")
-        half2 = keep.tile([P, TT, HALF], F32, name="half2")
-        nc.scalar.activation(out=half[:], in_=nfrac[:], func=ACT.Sin, scale=math.pi)
-        nc.scalar.activation(out=table[:, :, 1, 0, :], in_=nfrac[:], func=ACT.Sin, scale=-2.0 * math.pi)
-        nc.scalar.activation(out=table[:, :, 1, 1, :], in_=nfrac[:], func=ACT.Sin, scale=2.0 * math.pi)
-        nc.vector.scalar_tensor_tensor(
-            out=half2[:], in0=half[:], scalar=-2.0, in1=half[:], op0=ALU.mult, op1=ALU.mult
-        )
-        for j in range(2):
-            nc.vector.tensor_scalar(
-                out=table[:, :, 0, j, :], in0=half2[:], scalar1=1.0, scalar2=None, op0=ALU.add
+                k_tile = keep.tile([P, 4, 1024], BF16, name="k_raw%d" % g, tag="big", bufs=4)
+                load_w(k_tile[:], w_rk, g)
+                k_raw.append(k_tile)
+            whole = keep.tile([P, TT, HALF], I32, name="whole")
+            nc.vector.tensor_copy(out=whole[:], in_=turns[:])
+            frac = keep.tile([P, TT, HALF], F32, name="frac")
+            nc.vector.tensor_tensor(out=frac[:], in0=turns[:], in1=whole[:], op=ALU.subtract)
+            nfrac = keep.tile([P, TT, HALF], F32, name="nfrac")
+            nc.vector.scalar_tensor_tensor(
+                out=nfrac[:], in0=frac[:], scalar=0.5, in1=frac[:], op0=ALU.is_gt, op1=ALU.subtract
             )
-        for t in range(TT):
-            c_step(t)
-        dec_prep(qd_op, qd_raw, 0)
-        dec_prep(qd_op, qd_raw, 1)
-        rq_prep(1, 0)
-        dec_out(qd_op, q_rows, 0)
-        rq_prep(2, 0)
-        rq_prep(3, 0)
-        dec_out(qd_op, q_rows, 1)
-        rq_prep(0, 1)
-        rq_prep(1, 1)
-        rope_out(rq_op, q_rows, 0)
-        rq_prep(2, 1)
-        rq_prep(3, 1)
-        dec_prep(kd_op, kd_raw, 0)
-        dec_prep(kd_op, kd_raw, 1)
-        dec_out(kd_op, k_rows, 0)
-        rk_prep(0, 0)
-        rk_prep(1, 0)
-        rope_out(rq_op, q_rows, 1)
-        rk_prep(2, 0)
-        rk_prep(3, 0)
-        dec_out(kd_op, k_rows, 1)
-        rk_prep(0, 1)
-        rk_prep(1, 1)
-        rope_out(rk_op, k_rows, 0)
-        rk_prep(2, 1)
-        rk_prep(3, 1)
-        rope_out(rk_op, k_rows, 1)
+            half = keep.tile([P, TT, HALF], F32, name="half")
+            half2 = keep.tile([P, TT, HALF], F32, name="half2")
+            nc.scalar.activation(out=half[:], in_=nfrac[:], func=ACT.Sin, scale=math.pi)
+            nc.scalar.activation(out=table[:, :, 1, 0, :], in_=nfrac[:], func=ACT.Sin, scale=-2.0 * math.pi)
+            nc.scalar.activation(out=table[:, :, 1, 1, :], in_=nfrac[:], func=ACT.Sin, scale=2.0 * math.pi)
+            nc.vector.scalar_tensor_tensor(
+                out=half2[:], in0=half[:], scalar=-2.0, in1=half[:], op0=ALU.mult, op1=ALU.mult
+            )
+            for j in range(2):
+                nc.vector.tensor_scalar(
+                    out=table[:, :, 0, j, :], in0=half2[:], scalar1=1.0, scalar2=None, op0=ALU.add
+                )
+            c_mm(0)
+            c_mm(1)
+            turn(units[1], V_COLS[1])
+            c_quant(0)
+        last_out = None
+        for s in range(n):
+            unit = units[s]
+            unit_quant(unit)
+            if last_out is not None:
+                add_store(last_out)
+                last_out = None
+            if s == 0:
+                c_mm(2)
+                c_quant(1)
+                c_mm(3)
+            if s == 1:
+                c_quant(2)
+            if s + 2 < n:
+                turn(units[s + 2], V_COLS[s + 2])
+            if s == 1:
+                c_quant(3)
+            if unit[:2] == ("rk", 1):
+                for t in range(TT):
+                    mm("rk", 1, t, unit[2])
+            if s + 1 in outs:
+                mm_pair(outs[s + 1])
+            if s in outs:
+                out = outs[s]
+                plain(out, 0)
+                plain(out, 1)
+                products(out, 0)
+                products(out, 1)
+                last_out = out
+            if s in widen_at:
+                widen(*widen_at[s])
+        for pair in range(2):
+            out = ("rk", 1, pair)
+            plain(out, 0)
+            plain(out, 1)
+            products(out, 0)
+            products(out, 1)
+            add_store(out)

@@ -22,8 +22,12 @@ TT = S // P
 NG = D // 512
 FLOPS = 2 * (S * D * LQK + 2 * S * LQK * H * C + 2 * S * D * H * R)
 
-V_COLS = [320,320,0,0,0,0,256,256,0,0,0,0,96,96,96,96,96,96,256,256]
-V_PLANES = [1,2,2,2]
+V_COLS = [0,256,480,192,384,0,512,160,416,448,128,256,256,480,64,192,0,448,0,0]
+UNITS = [("qd", 0, 0), ("qd", 1, 0), ("kd", 0, 0), ("rq", 0, 0), ("rq", 1, 0), ("rk", 0, 1), ("rk", 0, 0), ("rq", 0, 1), ("rq", 1, 1), ("rk", 0, 2), ("rk", 0, 3), ("kd", 1, 0), ("rq", 0, 2), ("rq", 1, 2), ("rq", 0, 3), ("rq", 1, 3), ("rk", 1, 0), ("rk", 1, 3), ("rk", 1, 2), ("rk", 1, 1)]
+OUTS = {"qd":[1,2,4,9],"kd":[8,10,12,13],"rq":[15,16,18,22],"rk":[11,14,20,21]}
+WIDEN = [-5,-4,-2,-5,1,0,1,2,8,6,8,6,8,2,5,10]
+PE_UNITS = [("rk", 1, 3)]
+V_PLANES = [2,4,2,0]
 
 
 def tile_multiheadlatentattention_pa_kernel(
@@ -34,6 +38,7 @@ def tile_multiheadlatentattention_pa_kernel(
         keep = ctx.enter_context(tc.tile_pool(name="keep", bufs=1))
         work = ctx.enter_context(tc.tile_pool(name="work", bufs=3))
         psum = ctx.enter_context(tc.psum_pool(name="psum", bufs=8))
+        ctx.enter_context(tc.manual_schedule())
 
         warm = keep.tile([P, 1], F32, name="warm")
         nc.gpsimd.memset(warm[:], 0.0)
@@ -64,29 +69,37 @@ def tile_multiheadlatentattention_pa_kernel(
         nc.scalar.dma_start(
             out=q_scale[:], in_=w_rq_scale.rearrange("(g p t) o -> p g (t o)", p=P, t=4)
         )
+        load_w(c_pair[0][:, 0], w_c, 0)
         load_w(qb_raw[0][:], w_rq_bytes, 0)
-        for i in range(4):
+        load_w(c_pair[0][:, 1], w_c, 1)
+        load_x(0)
+        load_x(1)
+        for i in range(2, 4):
             load_w(c_pair[i // 2][:, i % 2], w_c, i)
             load_x(i)
         load_w(qd_raw[:], w_qd, 0)
         load_w(qb_raw[1][:], w_rq_bytes, 1)
         load_w(kd_raw[:], w_kd, 0)
         load_w(qb_raw[2][:], w_rq_bytes, 2)
-        load_w(qb_raw[3][:], w_rq_bytes, 3)
 
         pos = keep.tile([P, TT, 1], F32, name="pos")
         nc.gpsimd.iota(
             pos[:], pattern=[[P, TT], [0, 1]], base=0, channel_multiplier=1, allow_small_or_imprecise_dtypes=True
         )
         turns = keep.tile([P, TT, HALF], F32, name="turns")
-        for i in range(HALF):
-            nc.gpsimd.tensor_scalar(
-                out=turns[:, :, i : i + 1],
-                in0=pos[:],
-                scalar1=1.0 / (10000.0 ** (2.0 * i / R)) / (2.0 * math.pi),
+        nc.vector.tensor_scalar(
+            out=turns[:, :, 0:1], in0=pos[:], scalar1=1.0 / (2.0 * math.pi), scalar2=None, op0=ALU.mult
+        )
+        done = 1
+        while done < HALF:
+            nc.vector.tensor_scalar(
+                out=turns[:, :, done : 2 * done],
+                in0=turns[:, :, 0:done],
+                scalar1=10000.0 ** (-2.0 * done / R),
                 scalar2=None,
                 op0=ALU.mult,
             )
+            done *= 2
         table = keep.tile([P, TT, 2, 2, HALF], F32, name="table")
 
         def operand(name, parts, width):
@@ -110,7 +123,7 @@ def tile_multiheadlatentattention_pa_kernel(
         xgs = {}
 
         def x_turn(t):
-            xg = work.tile([P, NG * P * 4], BF16, name="xg", tag="stage", bufs=6, align_bytes=64)
+            xg = work.tile([P, NG * P * 4], BF16, name="xg", tag="stage", bufs=8, align_bytes=64)
             words = x_pair[t // 2][:, t % 2].bitcast(F32)
             xw = xg[:].bitcast(F32).rearrange("p (g r u) -> p g r u", g=NG, u=2)
             for b in range(2):
@@ -134,7 +147,7 @@ def tile_multiheadlatentattention_pa_kernel(
         cgs = {}
 
         def cw_turn(g):
-            grouped = work.tile([P, 512 * 4], BF16, name="cgrouped", tag="stage", bufs=6, align_bytes=64)
+            grouped = work.tile([P, 512 * 4], BF16, name="cgrouped", tag="stage", bufs=8, align_bytes=64)
             nc.vector.tensor_copy(
                 out=grouped[:].rearrange("p (t m j) -> p t m j", t=4, j=4),
                 in_=c_pair[g // 2][:, g % 2].rearrange("p j (m t) -> p t m j", t=4),
@@ -195,25 +208,36 @@ def tile_multiheadlatentattention_pa_kernel(
                 return k_raw[g][:, :, cols_of(half_no)]
             return {"qd": qd_raw, "kd": kd_raw}[kind][:, :, cols_of(half_no)]
 
+        planes = {}
+
+        def pe_turn(unit):
+            if unit[0] != "rq" and unit not in PE_UNITS:
+                return
+            raw = source(unit)
+            banks = []
+            for b in range(2):
+                pb = psum.tile([P, 2, 512], BF16, name="pbank", tag="bank")
+                for e in range(2):
+                    n0 = b * 256 + e * P
+                    nc.tensor.matmul(
+                        out=pb[:, e, :].rearrange("p (n t) -> p n t", t=4),
+                        lhsT=ident_b[:],
+                        rhs=raw[:, :, n0 : n0 + P].rearrange("p t n -> p n t"),
+                        start=True,
+                        stop=True,
+                    )
+                banks.append(pb)
+            planes[unit] = banks
+
         def turn(unit, v_cols):
             raw = source(unit)
-            grouped = work.tile([P, 512, 4], BF16, name="grouped", tag="stage", bufs=6, align_bytes=64)
+            grouped = work.tile([P, 512, 4], BF16, name="grouped", tag="stage", bufs=8, align_bytes=64)
             groups[unit] = grouped
-            if unit[0] == "rq":
+            if unit in planes:
                 for b in range(2):
-                    pb = psum.tile([P, 2, 512], BF16, name="pbank", tag="bank")
-                    for e in range(2):
-                        n0 = b * 256 + e * P
-                        nc.tensor.matmul(
-                            out=pb[:, e, :].rearrange("p (n t) -> p n t", t=4),
-                            lhsT=ident_b[:],
-                            rhs=raw[:, :, n0 : n0 + P].rearrange("p t n -> p n t"),
-                            start=True,
-                            stop=True,
-                        )
                     nc.scalar.copy(
                         out=grouped[:, b * 256 : b * 256 + 256, :].rearrange("p n t -> p (n t)"),
-                        in_=pb[:].rearrange("p e c -> p (e c)"),
+                        in_=planes[unit][b][:].rearrange("p e c -> p (e c)"),
                     )
                 return
             for eng, lo, hi in ((nc.vector.tensor_copy, 0, v_cols), (nc.scalar.copy, v_cols, 512)):
@@ -236,11 +260,11 @@ def tile_multiheadlatentattention_pa_kernel(
         prods = {}
         ress = {}
 
-        def mm(kind, half_no, t, g):
+        def mm(kind, half_no, t, g, first, final):
             op = ops[kind]
             cols = cols_of(half_no)
             last = 0 if kind in ("qd", "kd") else NG - 1
-            if g == 0:
+            if first:
                 acc = psum.tile([P, 512], F32, name="bank")
                 accs[(kind, half_no, t)] = acc
             src, part = (c_op, t) if last == 0 else (x_op, t * NG + g)
@@ -250,15 +274,16 @@ def tile_multiheadlatentattention_pa_kernel(
                 lhsT_scale=src[1][:, part, :],
                 rhs=op[0][:, g, cols].bitcast(FP8X4),
                 rhs_scale=op[1][:, g, cols],
-                start=(g == 0),
-                stop=(g == last),
+                start=first,
+                stop=final,
             )
 
         def mm_pair(out):
             kind, half_no, pair = out
             for e in range(2):
-                for g in range(1 if kind in ("qd", "kd") else NG):
-                    mm(kind, half_no, 2 * pair + e, g)
+                passes = 1 if kind in ("qd", "kd") else NG
+                for g in range(passes):
+                    mm(kind, half_no, 2 * pair + e, g, g == 0, g == passes - 1)
 
         def heads(out, e):
             kind, half_no, pair = out
@@ -301,72 +326,70 @@ def tile_multiheadlatentattention_pa_kernel(
                 in_=res[:].rearrange("p e h d -> p e (h d)"),
             )
 
-        units = [("qd", 0, 0), ("qd", 1, 0)]
-        units += [("rq", half_no, g) for g in range(2) for half_no in range(2)]
-        units += [("kd", 0, 0), ("kd", 1, 0)]
-        units += [("rq", half_no, g) for g in range(2, 4) for half_no in range(2)]
-        units += [("rk", half_no, g) for half_no in range(2) for g in range(NG)]
-        n = len(units)
+        whole = keep.tile([P, TT, HALF], I32, name="whole")
+        nc.vector.tensor_copy(out=whole[:], in_=turns[:])
+        frac = keep.tile([P, TT, HALF], F32, name="frac")
+        nc.vector.tensor_tensor(out=frac[:], in0=turns[:], in1=whole[:], op=ALU.subtract)
+        nfrac = keep.tile([P, TT, HALF], F32, name="nfrac")
+        nc.vector.scalar_tensor_tensor(
+            out=nfrac[:], in0=frac[:], scalar=0.5, in1=frac[:], op0=ALU.is_gt, op1=ALU.subtract
+        )
+        half = keep.tile([P, TT, HALF], F32, name="half")
+        half2 = keep.tile([P, TT, HALF], F32, name="half2")
+        nc.scalar.activation(out=half[:], in_=nfrac[:], func=ACT.Sin, scale=math.pi)
+        nc.scalar.activation(out=table[:, :, 1, 0, :], in_=nfrac[:], func=ACT.Sin, scale=-2.0 * math.pi)
+        nc.scalar.activation(out=table[:, :, 1, 1, :], in_=nfrac[:], func=ACT.Sin, scale=2.0 * math.pi)
+        nc.vector.scalar_tensor_tensor(
+            out=half2[:], in0=half[:], scalar=-2.0, in1=half[:], op0=ALU.mult, op1=ALU.mult
+        )
+        for j in range(2):
+            nc.vector.tensor_scalar(
+                out=table[:, :, 0, j, :], in0=half2[:], scalar1=1.0, scalar2=None, op0=ALU.add
+            )
+        n = len(UNITS)
         outs = {}
-        for s, out in enumerate([("qd", h, p) for h in range(2) for p in range(2)]):
-            outs[2 + s] = out
-        for s, out in enumerate([("kd", h, p) for h in range(2) for p in range(2)]):
-            outs[8 + s] = out
-        for s, out in enumerate([("rq", h, p) for h in range(2) for p in range(2)]):
-            outs[12 + s] = out
-        for s, out in enumerate([("rk", 0, p) for p in range(2)]):
-            outs[16 + s] = out
-        widen_at = {0: (1, (0, 1)), 1: (1, (2, 3)), 4: (2, (0, 1)), 5: (2, (2, 3)), 6: (3, (0, 1)), 7: (3, (2, 3))}
+        for kind in OUTS:
+            for i, s in enumerate(OUTS[kind]):
+                outs[s] = (kind, i // 2, i % 2)
+        k_raw = {}
 
-        with tc.manual_schedule():
-            widen(0, (0, 1))
-            for i in range(4):
-                cw_turn(i)
-                x_turn(i)
-                if i == 0:
-                    widen(0, (2, 3))
-                if i > 0:
-                    cw_quant(i - 1)
-                    x_quant(i - 1)
-            turn(units[0], V_COLS[0])
-            cw_quant(3)
-            x_quant(3)
-            k_raw = []
-            for g in range(NG):
-                k_tile = keep.tile([P, 4, 1024], BF16, name="k_raw%d" % g, tag="big", bufs=4)
-                load_w(k_tile[:], w_rk, g)
-                k_raw.append(k_tile)
-            whole = keep.tile([P, TT, HALF], I32, name="whole")
-            nc.vector.tensor_copy(out=whole[:], in_=turns[:])
-            frac = keep.tile([P, TT, HALF], F32, name="frac")
-            nc.vector.tensor_tensor(out=frac[:], in0=turns[:], in1=whole[:], op=ALU.subtract)
-            nfrac = keep.tile([P, TT, HALF], F32, name="nfrac")
-            nc.vector.scalar_tensor_tensor(
-                out=nfrac[:], in0=frac[:], scalar=0.5, in1=frac[:], op0=ALU.is_gt, op1=ALU.subtract
-            )
-            half = keep.tile([P, TT, HALF], F32, name="half")
-            half2 = keep.tile([P, TT, HALF], F32, name="half2")
-            nc.scalar.activation(out=half[:], in_=nfrac[:], func=ACT.Sin, scale=math.pi)
-            nc.scalar.activation(out=table[:, :, 1, 0, :], in_=nfrac[:], func=ACT.Sin, scale=-2.0 * math.pi)
-            nc.scalar.activation(out=table[:, :, 1, 1, :], in_=nfrac[:], func=ACT.Sin, scale=2.0 * math.pi)
-            nc.vector.scalar_tensor_tensor(
-                out=half2[:], in0=half[:], scalar=-2.0, in1=half[:], op0=ALU.mult, op1=ALU.mult
-            )
-            for j in range(2):
-                nc.vector.tensor_scalar(
-                    out=table[:, :, 0, j, :], in0=half2[:], scalar1=1.0, scalar2=None, op0=ALU.add
-                )
-            c_mm(0)
-            c_mm(1)
-            turn(units[1], V_COLS[1])
-            c_quant(0)
-        last_out = None
-        for s in range(n):
-            unit = units[s]
-            unit_quant(unit)
-            if last_out is not None:
-                add_store(last_out)
-                last_out = None
+        def load_k(g):
+            k_tile = keep.tile([P, 4, 1024], BF16, name="k_raw%d" % g, tag="big", bufs=4)
+            load_w(k_tile[:], w_rk, g)
+            k_raw[g] = k_tile
+
+        def widen_at(s):
+            for i in range(16):
+                if WIDEN[i] == s:
+                    widen(i // 4, (i % 4,))
+
+        for i in range(4):
+            cw_turn(i)
+            if i == 0:
+                widen_at(-5)
+            if i > 0:
+                cw_quant(i - 1)
+                x_quant(i - 1)
+            x_turn(i)
+            widen_at(i - 4)
+        turn(UNITS[0], V_COLS[0])
+        cw_quant(3)
+        x_quant(3)
+        for g in range(2):
+            load_k(g)
+        load_w(qb_raw[3][:], w_rq_bytes, 3)
+        for g in range(2, 4):
+            load_k(g)
+        c_mm(0)
+        c_mm(1)
+        turn(UNITS[1], V_COLS[1])
+        pe_turn(UNITS[2])
+        c_quant(0)
+        for s in range(n + 5):
+            if s < n:
+                unit_quant(UNITS[s])
+            if s - 2 in outs:
+                add_store(outs[s - 2])
             if s == 0:
                 c_mm(2)
                 c_quant(1)
@@ -374,27 +397,21 @@ def tile_multiheadlatentattention_pa_kernel(
             if s == 1:
                 c_quant(2)
             if s + 2 < n:
-                turn(units[s + 2], V_COLS[s + 2])
+                turn(UNITS[s + 2], V_COLS[s + 2])
+            if s + 3 < n:
+                pe_turn(UNITS[s + 3])
             if s == 1:
                 c_quant(3)
-            if unit[:2] == ("rk", 1):
-                for t in range(TT):
-                    mm("rk", 1, t, unit[2])
-            if s + 1 in outs:
-                mm_pair(outs[s + 1])
+            if s - 1 in outs:
+                products(outs[s - 1], 0)
+                products(outs[s - 1], 1)
             if s in outs:
-                out = outs[s]
-                plain(out, 0)
-                plain(out, 1)
-                products(out, 0)
-                products(out, 1)
-                last_out = out
-            if s in widen_at:
-                widen(*widen_at[s])
-        for pair in range(2):
-            out = ("rk", 1, pair)
-            plain(out, 0)
-            plain(out, 1)
-            products(out, 0)
-            products(out, 1)
-            add_store(out)
+                plain(outs[s], 0)
+                plain(outs[s], 1)
+            if s == n - 2 or s == n - 1:
+                for unit in UNITS[n - 4 : n - 1] if s == n - 2 else UNITS[n - 1 :]:
+                    for t in range(TT):
+                        mm(unit[0], unit[1], t, unit[2], unit == UNITS[n - 4], unit == UNITS[n - 1])
+            if s + 1 in outs and outs[s + 1][:2] != UNITS[n - 1][:2]:
+                mm_pair(outs[s + 1])
+            widen_at(s)

@@ -22,12 +22,55 @@ TT = S // P
 NG = D // 512
 FLOPS = 2 * (S * D * LQK + 2 * S * LQK * H * C + 2 * S * D * H * R)
 
-V_COLS = [0,256,480,192,384,0,512,160,416,448,128,256,256,480,64,192,0,448,0,0]
-UNITS = [("qd", 0, 0), ("qd", 1, 0), ("kd", 0, 0), ("rq", 0, 0), ("rq", 1, 0), ("rk", 0, 1), ("rk", 0, 0), ("rq", 0, 1), ("rq", 1, 1), ("rk", 0, 2), ("rk", 0, 3), ("kd", 1, 0), ("rq", 0, 2), ("rq", 1, 2), ("rq", 0, 3), ("rq", 1, 3), ("rk", 1, 0), ("rk", 1, 3), ("rk", 1, 2), ("rk", 1, 1)]
-OUTS = {"qd":[1,2,4,9],"kd":[8,10,12,13],"rq":[15,16,18,22],"rk":[11,14,20,21]}
-WIDEN = [-5,-4,-2,-5,1,0,1,2,8,6,8,6,8,2,5,10]
-PE_UNITS = [("rk", 1, 3)]
-V_PLANES = [2,4,2,0]
+PLAN = [
+    ("qd", 0, 0, 0),
+    ("qd", 1, 0, 512),
+    ("kd", 0, 0, 512),
+    ("rq", 0, 0, 512),
+    ("rq", 1, 0, 512),
+    ("rk", 0, 0, 384),
+    ("kd", 1, 0, 256),
+    ("rk", 0, 1, 512),
+    ("rk", 0, 2, 0),
+    ("rk", 0, 3, 384),
+    ("rq", 1, 1, 0),
+    ("rq", 0, 1, 0),
+    ("rq", 0, 2, 256),
+    ("rq", 0, 3, 0),
+    ("rq", 1, 2, 0),
+    ("rq", 1, 3, 256),
+    ("rk", 1, 0, 0),
+    ("rk", 1, 2, 256),
+    ("rk", 1, 3, 0),
+    ("rk", 1, 1, 0),
+]
+OUTS = {
+    1: ("qd", 0, 0),
+    2: ("qd", 0, 1),
+    5: ("qd", 1, 0),
+    8: ("kd", 0, 0),
+    9: ("kd", 0, 1),
+    11: ("kd", 1, 0),
+    12: ("kd", 1, 1),
+    13: ("qd", 1, 1),
+    14: ("rk", 0, 0),
+    15: ("rk", 0, 1),
+    16: ("rq", 0, 0),
+    18: ("rq", 0, 1),
+    19: ("rq", 1, 0),
+    20: ("rk", 1, 0),
+    21: ("rk", 1, 1),
+    22: ("rq", 1, 1),
+}
+WIDEN = {
+    -5: ((0, 0, "vector"), (0, 1, "scalar"), (0, 2, "scalar"),),
+    -4: ((0, 3, "scalar"),),
+    0: ((1, 0, "vector"), (1, 2, "scalar"),),
+    3: ((1, 1, "scalar"), (1, 3, "scalar"), (3, 1, "vector"),),
+    5: ((3, 3, "scalar"),),
+    8: ((3, 2, "vector"),),
+    9: ((2, 0, "vector"), (2, 1, "vector"), (2, 2, "scalar"), (2, 3, "scalar"), (3, 0, "vector"),),
+}
 
 
 def tile_multiheadlatentattention_pa_kernel(
@@ -40,52 +83,49 @@ def tile_multiheadlatentattention_pa_kernel(
         psum = ctx.enter_context(tc.psum_pool(name="psum", bufs=8))
         ctx.enter_context(tc.manual_schedule())
 
-        warm = keep.tile([P, 1], F32, name="warm")
-        nc.gpsimd.memset(warm[:], 0.0)
-        warm2 = keep.tile([P, 1], F32, name="warm2")
-        nc.scalar.activation(out=warm2[:], in_=warm[:], func=ACT.Sin)
-        ident = keep.tile([P, P], F32, name="ident")
-        make_identity(nc, ident[:])
-        ident_b = keep.tile([P, P], BF16, name="ident_b")
-        make_identity(nc, ident_b[:])
-
         x_pair = [keep.tile([P, 2, D], BF16, name="x_pair%d" % t, tag="big", bufs=4) for t in range(2)]
         c_pair = [keep.tile([P, 2, 4, 512], BF16, name="c_pair%d" % t, tag="big", bufs=4) for t in range(2)]
         qb_raw = [keep.tile([P, 4, 1024], U8, name="qb_raw%d" % g) for g in range(NG)]
         qd_raw = keep.tile([P, 4, 1024], BF16, name="qd_raw")
         kd_raw = keep.tile([P, 4, 1024], BF16, name="kd_raw")
-        q_scale = keep.tile([P, NG, 4], F32, name="q_scale")
-
+        q_scale = [keep.tile([P, 4], F32, name="q_scale%d" % g) for g in range(NG)]
         x_rows = x.rearrange("b s d -> (b s) d")
 
         def load_x(t):
             nc.sync.dma_start(out=x_pair[t // 2][:, t % 2], in_=x_rows[t * P : (t + 1) * P, :])
 
         def load_w(dst, src, g):
-            nc.sync.dma_start(
-                out=dst, in_=src[g * 512 : (g + 1) * 512, :].rearrange("(p t) n -> p t n", t=4)
-            )
+            nc.sync.dma_start(out=dst, in_=src[g * 512 : (g + 1) * 512, :].rearrange("(p t) n -> p t n", t=4))
 
-        nc.scalar.dma_start(
-            out=q_scale[:], in_=w_rq_scale.rearrange("(g p t) o -> p g (t o)", p=P, t=4)
-        )
+        def load_scale(g):
+            rows = w_rq_scale[g * 512 : (g + 1) * 512, :]
+            nc.scalar.dma_start(out=q_scale[g][:], in_=rows.rearrange("(p t) o -> p (t o)", t=4))
+
+        load_scale(0)
         load_w(c_pair[0][:, 0], w_c, 0)
         load_w(qb_raw[0][:], w_rq_bytes, 0)
         load_w(c_pair[0][:, 1], w_c, 1)
         load_x(0)
         load_x(1)
         for i in range(2, 4):
-            load_w(c_pair[i // 2][:, i % 2], w_c, i)
+            load_w(c_pair[1][:, i % 2], w_c, i)
             load_x(i)
         load_w(qd_raw[:], w_qd, 0)
         load_w(qb_raw[1][:], w_rq_bytes, 1)
         load_w(kd_raw[:], w_kd, 0)
         load_w(qb_raw[2][:], w_rq_bytes, 2)
 
+        zero = keep.tile([P, 1], F32, name="zero")
+        nc.gpsimd.memset(zero[:], 0.0)
+        sin_zero = keep.tile([P, 1], F32, name="sin_zero")
+        nc.scalar.activation(out=sin_zero[:], in_=zero[:], func=ACT.Sin)
         pos = keep.tile([P, TT, 1], F32, name="pos")
         nc.gpsimd.iota(
             pos[:], pattern=[[P, TT], [0, 1]], base=0, channel_multiplier=1, allow_small_or_imprecise_dtypes=True
         )
+        ident = keep.tile([P, P], F32, name="ident")
+        make_identity(nc, ident[:])
+
         turns = keep.tile([P, TT, HALF], F32, name="turns")
         nc.vector.tensor_scalar(
             out=turns[:, :, 0:1], in0=pos[:], scalar1=1.0 / (2.0 * math.pi), scalar2=None, op0=ALU.mult
@@ -100,34 +140,54 @@ def tile_multiheadlatentattention_pa_kernel(
                 op0=ALU.mult,
             )
             done *= 2
+        whole = keep.tile([P, TT, HALF], I32, name="whole")
+        nc.vector.tensor_copy(out=whole[:], in_=turns[:])
+        frac = keep.tile([P, TT, HALF], F32, name="frac")
+        nc.vector.tensor_tensor(out=frac[:], in0=turns[:], in1=whole[:], op=ALU.subtract)
+        nfrac = keep.tile([P, TT, HALF], F32, name="nfrac")
+        nc.vector.scalar_tensor_tensor(
+            out=nfrac[:], in0=frac[:], scalar=0.5, in1=frac[:], op0=ALU.is_gt, op1=ALU.subtract
+        )
+        half_sin = keep.tile([P, TT, HALF], F32, name="half_sin")
+        nc.scalar.activation(out=half_sin[:], in_=nfrac[:], func=ACT.Sin, scale=math.pi)
         table = keep.tile([P, TT, 2, 2, HALF], F32, name="table")
+        for j, sign in enumerate((-1.0, 1.0)):
+            nc.scalar.activation(out=table[:, :, 1, j, :], in_=nfrac[:], func=ACT.Sin, scale=sign * 2.0 * math.pi)
+        dcos = keep.tile([P, TT, HALF], F32, name="dcos")
+        nc.vector.scalar_tensor_tensor(
+            out=dcos[:], in0=half_sin[:], scalar=-2.0, in1=half_sin[:], op0=ALU.mult, op1=ALU.mult
+        )
+        for j in range(2):
+            nc.vector.tensor_scalar(out=table[:, :, 0, j, :], in0=dcos[:], scalar1=1.0, scalar2=None, op0=ALU.add)
 
         def operand(name, parts, width):
             codes = keep.tile([P, parts, width], U32, name=name + "_codes", align_bytes=64)
             scales = keep.tile([P, parts, width], U8, name=name + "_scales", align_bytes=64)
             return codes, scales
 
-        x_op = operand("x", TT * NG, P)
-        c_w_op = operand("c_w", NG, 512)
-        c_op = operand("c", TT, P)
-        qd_op = operand("qd", 1, 1024)
-        kd_op = operand("kd", 1, 1024)
-        rq_op = operand("rq", NG, 1024)
-        rk_op = operand("rk", NG, 1024)
-
         def quantize(op, part, cols, grouped):
             nc.vector.quantize_mx(
                 out=op[0][:, part, cols].bitcast(FP8X4), scales=op[1][:, part, cols], in_=grouped
             )
 
-        xgs = {}
+        x_op = operand("x", TT * NG, P)
+        c_w_op = operand("c_w", NG, 512)
+        c_op = operand("c", TT, P)
+        ops = {
+            "qd": operand("qd", 1, 1024),
+            "kd": operand("kd", 1, 1024),
+            "rq": operand("rq", NG, 1024),
+            "rk": operand("rk", NG, 1024),
+        }
+
+        staged = {}
 
         def x_turn(t):
             xg = work.tile([P, NG * P * 4], BF16, name="xg", tag="stage", bufs=8, align_bytes=64)
             words = x_pair[t // 2][:, t % 2].bitcast(F32)
             xw = xg[:].bitcast(F32).rearrange("p (g r u) -> p g r u", g=NG, u=2)
             for b in range(2):
-                xt = psum.tile([P, 2, 2, P], F32, name="bank")
+                xt = psum.tile([P, 2, 2, P], F32, name="xt", tag="bank")
                 for e in range(2):
                     g = 2 * b + e
                     for u in range(2):
@@ -135,32 +195,29 @@ def tile_multiheadlatentattention_pa_kernel(
                             xt[:, e, u, :], words[:, 256 * g + u : 256 * (g + 1) : 2], ident[:]
                         )
                 nc.scalar.copy(out=xw[:, 2 * b : 2 * b + 2], in_=xt[:].rearrange("p g u r -> p g r u"))
-            xgs[t] = xg
+            staged[("x", t)] = xg
 
         def x_quant(t):
+            parts = slice(t * NG, (t + 1) * NG)
             nc.vector.quantize_mx(
-                out=x_op[0][:, t * NG : (t + 1) * NG, :].rearrange("p g n -> p (g n)").bitcast(FP8X4),
-                scales=x_op[1][:, t * NG : (t + 1) * NG, :].rearrange("p g n -> p (g n)"),
-                in_=xgs[t][:],
+                out=x_op[0][:, parts, :].rearrange("p g n -> p (g n)").bitcast(FP8X4),
+                scales=x_op[1][:, parts, :].rearrange("p g n -> p (g n)"),
+                in_=staged[("x", t)][:],
             )
 
-        cgs = {}
-
         def cw_turn(g):
-            grouped = work.tile([P, 512 * 4], BF16, name="cgrouped", tag="stage", bufs=8, align_bytes=64)
+            grouped = work.tile([P, 512 * 4], BF16, name="cw_grouped", tag="stage", bufs=8, align_bytes=64)
             nc.vector.tensor_copy(
                 out=grouped[:].rearrange("p (t m j) -> p t m j", t=4, j=4),
                 in_=c_pair[g // 2][:, g % 2].rearrange("p j (m t) -> p t m j", t=4),
             )
-            cgs[g] = grouped
+            staged[("c_w", g)] = grouped
 
         def cw_quant(g):
-            quantize(c_w_op, g, slice(0, 512), cgs[g][:])
-
-        lat = {}
+            quantize(c_w_op, g, slice(0, 512), staged[("c_w", g)][:])
 
         def c_mm(t):
-            cb = psum.tile([P, 4, P], F32, name="bank")
+            cb = psum.tile([P, 4, P], F32, name="cb", tag="bank")
             for j in range(4):
                 for g in range(NG):
                     nc.tensor.matmul_mx(
@@ -174,183 +231,15 @@ def tile_multiheadlatentattention_pa_kernel(
                     )
             cg = work.tile([P, P, 4], BF16, name="cg", bufs=2, align_bytes=64)
             nc.scalar.copy(out=cg[:], in_=cb[:].rearrange("p t n -> p n t"))
-            lat[t] = cg
+            staged[("c", t)] = cg
 
         def c_quant(t):
-            quantize(c_op, t, slice(0, P), lat[t][:].rearrange("p n t -> p (n t)"))
+            quantize(c_op, t, slice(0, P), staged[("c", t)][:].rearrange("p n t -> p (n t)"))
 
         def cols_of(half_no):
             return slice(half_no * 512, half_no * 512 + 512)
 
-        wides = {}
-        groups = {}
-
-        def widen(g, planes):
-            if g not in wides:
-                wide = work.tile([P, 4, 1024], BF16, name="wide", bufs=2, align_bytes=64)
-                wides[g] = wide
-            for j in planes:
-                src = qb_raw[g][:, j, :].bitcast(FP8)
-                if j < V_PLANES[g]:
-                    nc.vector.tensor_scalar(
-                        out=wides[g][:, j, :], in0=src, scalar1=q_scale[:, g, j : j + 1], scalar2=None, op0=ALU.mult
-                    )
-                else:
-                    nc.scalar.activation(
-                        out=wides[g][:, j, :], in_=src, func=ACT.Copy, scale=q_scale[:, g, j : j + 1]
-                    )
-
-        def source(unit):
-            kind, half_no, g = unit
-            if kind == "rq":
-                return wides[g][:, :, cols_of(half_no)]
-            if kind == "rk":
-                return k_raw[g][:, :, cols_of(half_no)]
-            return {"qd": qd_raw, "kd": kd_raw}[kind][:, :, cols_of(half_no)]
-
-        planes = {}
-
-        def pe_turn(unit):
-            if unit[0] != "rq" and unit not in PE_UNITS:
-                return
-            raw = source(unit)
-            banks = []
-            for b in range(2):
-                pb = psum.tile([P, 2, 512], BF16, name="pbank", tag="bank")
-                for e in range(2):
-                    n0 = b * 256 + e * P
-                    nc.tensor.matmul(
-                        out=pb[:, e, :].rearrange("p (n t) -> p n t", t=4),
-                        lhsT=ident_b[:],
-                        rhs=raw[:, :, n0 : n0 + P].rearrange("p t n -> p n t"),
-                        start=True,
-                        stop=True,
-                    )
-                banks.append(pb)
-            planes[unit] = banks
-
-        def turn(unit, v_cols):
-            raw = source(unit)
-            grouped = work.tile([P, 512, 4], BF16, name="grouped", tag="stage", bufs=8, align_bytes=64)
-            groups[unit] = grouped
-            if unit in planes:
-                for b in range(2):
-                    nc.scalar.copy(
-                        out=grouped[:, b * 256 : b * 256 + 256, :].rearrange("p n t -> p (n t)"),
-                        in_=planes[unit][b][:].rearrange("p e c -> p (e c)"),
-                    )
-                return
-            for eng, lo, hi in ((nc.vector.tensor_copy, 0, v_cols), (nc.scalar.copy, v_cols, 512)):
-                if hi > lo:
-                    eng(
-                        out=grouped[:, lo:hi, :].rearrange("p (c i) t -> p c t i", i=4),
-                        in_=raw[:, :, lo:hi].rearrange("p t (c i) -> p c t i", i=4),
-                    )
-
-        ops = {"qd": qd_op, "kd": kd_op, "rq": rq_op, "rk": rk_op}
-
-        def unit_quant(unit):
-            kind, half_no, g = unit
-            quantize(ops[kind], g, cols_of(half_no), groups[unit][:].rearrange("p n t -> p (n t)"))
-
-        q_rows = out_q.rearrange("b s h d -> (b s) (h d)").rearrange("(t p) c -> p t c", p=P)
-        k_rows = out_k.rearrange("b s h d -> (b s) (h d)").rearrange("(t p) c -> p t c", p=P)
-        rows_of = {"qd": q_rows, "kd": k_rows, "rq": q_rows, "rk": k_rows}
-        accs = {}
-        prods = {}
-        ress = {}
-
-        def mm(kind, half_no, t, g, first, final):
-            op = ops[kind]
-            cols = cols_of(half_no)
-            last = 0 if kind in ("qd", "kd") else NG - 1
-            if first:
-                acc = psum.tile([P, 512], F32, name="bank")
-                accs[(kind, half_no, t)] = acc
-            src, part = (c_op, t) if last == 0 else (x_op, t * NG + g)
-            nc.tensor.matmul_mx(
-                out=accs[(kind, half_no, t)][:],
-                lhsT=src[0][:, part, :].bitcast(FP8X4),
-                lhsT_scale=src[1][:, part, :],
-                rhs=op[0][:, g, cols].bitcast(FP8X4),
-                rhs_scale=op[1][:, g, cols],
-                start=first,
-                stop=final,
-            )
-
-        def mm_pair(out):
-            kind, half_no, pair = out
-            for e in range(2):
-                passes = 1 if kind in ("qd", "kd") else NG
-                for g in range(passes):
-                    mm(kind, half_no, 2 * pair + e, g, g == 0, g == passes - 1)
-
-        def heads(out, e):
-            kind, half_no, pair = out
-            return accs[(kind, half_no, 2 * pair + e)][:].rearrange("p (h d) -> p h d", h=4)
-
-        def products(out, e):
-            if e == 0:
-                prod = work.tile([P, 2, 2, 4, R], F32, name="prod", bufs=3)
-                prods[out] = prod
-            nc.vector.tensor_tensor(
-                out=prods[out][:, :, e],
-                in0=heads(out, e)[:, :, C:DH].unsqueeze(1).to_broadcast([P, 2, 4, R]),
-                in1=table[:, 2 * out[2] + e]
-                .rearrange("p c j i -> p c (j i)")
-                .unsqueeze(2)
-                .to_broadcast([P, 2, 4, R]),
-                op=ALU.mult,
-            )
-
-        def plain(out, e):
-            if e == 0:
-                res = work.tile([P, 2, 4, DH], F32, name="res", bufs=5)
-                ress[out] = res
-            nc.scalar.copy(out=ress[out][:, e, :, 0:C], in_=heads(out, e)[:, :, 0:C])
-
-        def add_store(out):
-            kind, half_no, pair = out
-            prod = prods[out]
-            res = ress[out]
-            p2 = prod[:, 1].rearrange("p e h (j i) -> p (e h) j i", j=2)
-            nc.vector.tensor_tensor(
-                out=res[:, :, :, C:DH].rearrange("p e h (j i) -> p (e h) j i", j=2),
-                in0=prod[:, 0].rearrange("p e h (j i) -> p (e h) j i", j=2),
-                in1=p2[:, :, ::-1, :],
-                op=ALU.add,
-            )
-            col0 = half_no * 512 + (0 if kind in ("qd", "kd") else 1024)
-            nc.sync.dma_start(
-                out=rows_of[kind][:, 2 * pair : 2 * pair + 2, col0 : col0 + 512],
-                in_=res[:].rearrange("p e h d -> p e (h d)"),
-            )
-
-        whole = keep.tile([P, TT, HALF], I32, name="whole")
-        nc.vector.tensor_copy(out=whole[:], in_=turns[:])
-        frac = keep.tile([P, TT, HALF], F32, name="frac")
-        nc.vector.tensor_tensor(out=frac[:], in0=turns[:], in1=whole[:], op=ALU.subtract)
-        nfrac = keep.tile([P, TT, HALF], F32, name="nfrac")
-        nc.vector.scalar_tensor_tensor(
-            out=nfrac[:], in0=frac[:], scalar=0.5, in1=frac[:], op0=ALU.is_gt, op1=ALU.subtract
-        )
-        half = keep.tile([P, TT, HALF], F32, name="half")
-        half2 = keep.tile([P, TT, HALF], F32, name="half2")
-        nc.scalar.activation(out=half[:], in_=nfrac[:], func=ACT.Sin, scale=math.pi)
-        nc.scalar.activation(out=table[:, :, 1, 0, :], in_=nfrac[:], func=ACT.Sin, scale=-2.0 * math.pi)
-        nc.scalar.activation(out=table[:, :, 1, 1, :], in_=nfrac[:], func=ACT.Sin, scale=2.0 * math.pi)
-        nc.vector.scalar_tensor_tensor(
-            out=half2[:], in0=half[:], scalar=-2.0, in1=half[:], op0=ALU.mult, op1=ALU.mult
-        )
-        for j in range(2):
-            nc.vector.tensor_scalar(
-                out=table[:, :, 0, j, :], in0=half2[:], scalar1=1.0, scalar2=None, op0=ALU.add
-            )
-        n = len(UNITS)
-        outs = {}
-        for kind in OUTS:
-            for i, s in enumerate(OUTS[kind]):
-                outs[s] = (kind, i // 2, i % 2)
+        wide_tiles = {}
         k_raw = {}
 
         def load_k(g):
@@ -359,37 +248,145 @@ def tile_multiheadlatentattention_pa_kernel(
             k_raw[g] = k_tile
 
         def widen_at(s):
-            for i in range(16):
-                if WIDEN[i] == s:
-                    widen(i // 4, (i % 4,))
+            for g, j, engine in WIDEN.get(s, ()):
+                if g not in wide_tiles:
+                    wide = work.tile([P, 4, 1024], BF16, name="wide", bufs=2, align_bytes=64)
+                    wide_tiles[g] = wide
+                dst = wide_tiles[g][:, j, :]
+                src = qb_raw[g][:, j, :].bitcast(FP8)
+                scale = q_scale[g][:, j : j + 1]
+                if engine == "vector":
+                    nc.vector.tensor_scalar(out=dst, in0=src, scalar1=scale, scalar2=None, op0=ALU.mult)
+                else:
+                    nc.scalar.activation(out=dst, in_=src, func=ACT.Copy, scale=scale)
+
+        def source(unit):
+            kind, half_no, g, v_cols = unit
+            raw = {"qd": qd_raw, "kd": kd_raw, "rq": wide_tiles.get(g), "rk": k_raw.get(g)}[kind]
+            return raw[:, :, cols_of(half_no)]
+
+        def turn(unit):
+            v_cols = unit[3]
+            grouped = work.tile([P, 512, 4], BF16, name="grouped", tag="stage", bufs=8, align_bytes=64)
+            staged[unit] = grouped
+            raw = source(unit)
+            for copy, lo, hi in ((nc.vector.tensor_copy, 0, v_cols), (nc.scalar.copy, v_cols, 512)):
+                if hi > lo:
+                    copy(
+                        out=grouped[:, lo:hi, :].rearrange("p (c i) t -> p c t i", i=4),
+                        in_=raw[:, :, lo:hi].rearrange("p t (c i) -> p c t i", i=4),
+                    )
+
+        def unit_quant(unit):
+            kind, half_no, g, v_cols = unit
+            quantize(ops[kind], g, cols_of(half_no), staged[unit][:].rearrange("p n t -> p (n t)"))
+
+        q_rows = out_q.rearrange("b s h d -> (b s) (h d)").rearrange("(t p) c -> p t c", p=P)
+        k_rows = out_k.rearrange("b s h d -> (b s) (h d)").rearrange("(t p) c -> p t c", p=P)
+        accs = {}
+        prods = {}
+        ress = {}
+
+        def passes_of(kind):
+            return 1 if kind in ("qd", "kd") else NG
+
+        def multiply(kind, half_no, t, g, first, last):
+            if first:
+                acc = psum.tile([P, 512], F32, name="acc", tag="bank")
+                accs[(kind, half_no, t)] = acc
+            moving = ops[kind]
+            fixed, part = (c_op, t) if passes_of(kind) == 1 else (x_op, t * NG + g)
+            nc.tensor.matmul_mx(
+                out=accs[(kind, half_no, t)][:],
+                lhsT=fixed[0][:, part, :].bitcast(FP8X4),
+                lhsT_scale=fixed[1][:, part, :],
+                rhs=moving[0][:, g, cols_of(half_no)].bitcast(FP8X4),
+                rhs_scale=moving[1][:, g, cols_of(half_no)],
+                start=first,
+                stop=last,
+            )
+
+        def multiply_pair(out):
+            kind, half_no, pair = out
+            passes = passes_of(kind)
+            for t in (2 * pair, 2 * pair + 1):
+                for g in range(passes):
+                    multiply(kind, half_no, t, g, g == 0, g == passes - 1)
+
+        def heads(out, e):
+            kind, half_no, pair = out
+            return accs[(kind, half_no, 2 * pair + e)][:].rearrange("p (h d) -> p h d", h=4)
+
+        def plain(out):
+            res = work.tile([P, 2, 4, DH], F32, name="res", bufs=5)
+            ress[out] = res
+            for e in range(2):
+                nc.scalar.copy(out=res[:, e, :, 0:C], in_=heads(out, e)[:, :, 0:C])
+
+        def products(out):
+            prod = work.tile([P, 2, 2, 4, R], F32, name="prod", bufs=3)
+            prods[out] = prod
+            for e in range(2):
+                nc.vector.tensor_tensor(
+                    out=prod[:, :, e],
+                    in0=heads(out, e)[:, :, C:DH].unsqueeze(1).to_broadcast([P, 2, 4, R]),
+                    in1=table[:, 2 * out[2] + e]
+                    .rearrange("p c j i -> p c (j i)")
+                    .unsqueeze(2)
+                    .to_broadcast([P, 2, 4, R]),
+                    op=ALU.mult,
+                )
+
+        def add_store(out, lo, hi):
+            kind, half_no, pair = out
+            terms = [prods[out][:, c, lo:hi].rearrange("p e h (j i) -> p (e h) j i", j=2) for c in range(2)]
+            nc.vector.tensor_tensor(
+                out=ress[out][:, lo:hi, :, C:DH].rearrange("p e h (j i) -> p (e h) j i", j=2),
+                in0=terms[0],
+                in1=terms[1][:, :, ::-1, :],
+                op=ALU.add,
+            )
+            rows = q_rows if kind in ("qd", "rq") else k_rows
+            col0 = half_no * 512 + (0 if passes_of(kind) == 1 else H * C)
+            nc.sync.dma_start(
+                out=rows[:, 2 * pair + lo : 2 * pair + hi, col0 : col0 + 512],
+                in_=ress[out][:, lo:hi].rearrange("p e h d -> p e (h d)"),
+            )
 
         for i in range(4):
             cw_turn(i)
             if i == 0:
                 widen_at(-5)
-            if i > 0:
+            else:
                 cw_quant(i - 1)
                 x_quant(i - 1)
             x_turn(i)
             widen_at(i - 4)
-        turn(UNITS[0], V_COLS[0])
+        turn(PLAN[0])
         cw_quant(3)
         x_quant(3)
-        for g in range(2):
-            load_k(g)
+        for g in range(1, NG):
+            load_scale(g)
+        load_k(0)
+        load_k(1)
         load_w(qb_raw[3][:], w_rq_bytes, 3)
-        for g in range(2, 4):
-            load_k(g)
+        load_k(2)
+        load_k(3)
         c_mm(0)
         c_mm(1)
-        turn(UNITS[1], V_COLS[1])
-        pe_turn(UNITS[2])
+        turn(PLAN[1])
         c_quant(0)
-        for s in range(n + 5):
+
+        n = len(PLAN)
+        final = PLAN[n - 4 :]
+        banks = 0
+        ready = set()
+        multiplied = set()
+        last_step = max(OUTS)
+        for s in range(last_step + 3):
             if s < n:
-                unit_quant(UNITS[s])
-            if s - 2 in outs:
-                add_store(outs[s - 2])
+                unit_quant(PLAN[s])
+                ready.add(PLAN[s][:3])
             if s == 0:
                 c_mm(2)
                 c_quant(1)
@@ -397,21 +394,36 @@ def tile_multiheadlatentattention_pa_kernel(
             if s == 1:
                 c_quant(2)
             if s + 2 < n:
-                turn(UNITS[s + 2], V_COLS[s + 2])
-            if s + 3 < n:
-                pe_turn(UNITS[s + 3])
+                turn(PLAN[s + 2])
             if s == 1:
                 c_quant(3)
-            if s - 1 in outs:
-                products(outs[s - 1], 0)
-                products(outs[s - 1], 1)
-            if s in outs:
-                plain(outs[s], 0)
-                plain(outs[s], 1)
-            if s == n - 2 or s == n - 1:
-                for unit in UNITS[n - 4 : n - 1] if s == n - 2 else UNITS[n - 1 :]:
+            if s - 1 in OUTS:
+                products(OUTS[s - 1])
+                banks -= 2
+            if s - 2 in OUTS:
+                if s - 2 == last_step:
+                    add_store(OUTS[s - 2], 0, 1)
+                    add_store(OUTS[s - 2], 1, 2)
+                else:
+                    add_store(OUTS[s - 2], 0, 2)
+            if s in OUTS:
+                plain(OUTS[s])
+            if s == n - 2:
+                banks += 4
+                for unit in final[:3]:
                     for t in range(TT):
-                        mm(unit[0], unit[1], t, unit[2], unit == UNITS[n - 4], unit == UNITS[n - 1])
-            if s + 1 in outs and outs[s + 1][:2] != UNITS[n - 1][:2]:
-                mm_pair(outs[s + 1])
+                        multiply(unit[0], unit[1], t, unit[2], unit == final[0], False)
+            if s == n - 1:
+                for t in range(TT):
+                    multiply(final[3][0], final[3][1], t, final[3][2], False, True)
+            for out in (OUTS.get(s + 1), OUTS.get(s + 2)):
+                if out is not None and out[:2] != final[0][:2] and out not in multiplied:
+                    kind, half_no, pair = out
+                    if banks + 2 > 8 or any((kind, half_no, g) not in ready for g in range(passes_of(kind))):
+                        break
+                    if passes_of(kind) == 1 and s < pair:
+                        break
+                    multiply_pair(out)
+                    multiplied.add(out)
+                    banks += 2
             widen_at(s)

@@ -15,62 +15,55 @@ ALU = mybir.AluOpType
 ACT = mybir.ActivationFunctionType
 
 P = 128
-S, D, H, DH, LQK, R = 512, 2048, 16, 128, 512, 64
-C = DH - R
-HALF = R // 2
-TT = S // P
-NG = D // 512
-FLOPS = 2 * (S * D * LQK + 2 * S * LQK * H * C + 2 * S * D * H * R)
+TOKENS, D_MODEL, HEADS, HEAD_DIM, LATENT, ROTATED = 512, 2048, 16, 128, 512, 64
+PLAIN = HEAD_DIM - ROTATED
+HALF = ROTATED // 2
+PASS = 512
+PASSES = D_MODEL // PASS
+TOKEN_TILES = TOKENS // P
+BANK = 512
+BANKS = 8
+WIDTH = 2 * BANK
+FLOPS = 2 * TOKENS * (D_MODEL * LATENT + 2 * LATENT * WIDTH + 2 * D_MODEL * WIDTH)
 
-PLAN = [
+UNITS = (
     ("qd", 0, 0, 0),
     ("qd", 1, 0, 512),
-    ("kd", 0, 0, 512),
+    ("kd", 0, 0, 128),
+    ("kd", 1, 0, 384),
     ("rq", 0, 0, 512),
-    ("rq", 1, 0, 512),
-    ("rk", 0, 0, 384),
-    ("kd", 1, 0, 256),
-    ("rk", 0, 1, 512),
-    ("rk", 0, 2, 0),
-    ("rk", 0, 3, 384),
-    ("rq", 1, 1, 0),
     ("rq", 0, 1, 0),
-    ("rq", 0, 2, 256),
-    ("rq", 0, 3, 0),
+    ("rq", 1, 0, 512),
+    ("rq", 1, 1, 0),
+    ("rk", 0, 0, 0),
+    ("rk", 0, 1, 512),
+    ("rk", 0, 2, 384),
+    ("rk", 0, 3, 512),
+    ("rq", 0, 2, 0),
+    ("rq", 0, 3, 512),
     ("rq", 1, 2, 0),
-    ("rq", 1, 3, 256),
+    ("rq", 1, 3, 0),
     ("rk", 1, 0, 0),
-    ("rk", 1, 2, 256),
+    ("rk", 1, 1, 256),
+    ("rk", 1, 2, 0),
     ("rk", 1, 3, 0),
-    ("rk", 1, 1, 0),
-]
-OUTS = {
-    1: ("qd", 0, 0),
-    2: ("qd", 0, 1),
-    5: ("qd", 1, 0),
-    8: ("kd", 0, 0),
-    9: ("kd", 0, 1),
-    11: ("kd", 1, 0),
-    12: ("kd", 1, 1),
-    13: ("qd", 1, 1),
-    14: ("rk", 0, 0),
-    15: ("rk", 0, 1),
-    16: ("rq", 0, 0),
-    18: ("rq", 0, 1),
-    19: ("rq", 1, 0),
-    20: ("rk", 1, 0),
-    21: ("rk", 1, 1),
-    22: ("rq", 1, 1),
+)
+
+OUTPUT_STEPS = {
+    "qd": (3, 5, 6, 7),
+    "kd": (8, 10, 11, 14),
+    "rk": (12, 13, 20, 21),
+    "rq": (16, 18, 19, 22),
 }
-WIDEN = {
-    -5: ((0, 0, "vector"), (0, 1, "scalar"), (0, 2, "scalar"),),
-    -4: ((0, 3, "scalar"),),
-    0: ((1, 0, "vector"), (1, 2, "scalar"),),
-    3: ((1, 1, "scalar"), (1, 3, "scalar"), (3, 1, "vector"),),
-    5: ((3, 3, "scalar"),),
-    8: ((3, 2, "vector"),),
-    9: ((2, 0, "vector"), (2, 1, "vector"), (2, 2, "scalar"), (2, 3, "scalar"), (3, 0, "vector"),),
+
+WIDEN_STEPS = {
+    4: ((3, 3),),
+    6: ((2, 0),),
+    7: ((2, 1), (2, 2)),
+    8: ((2, 3), (3, 0), (3, 1)),
+    9: ((3, 2),),
 }
+VECTOR_PLANES = ((3,), (1, 2, 3), (), (3,))
 
 
 def tile_multiheadlatentattention_pa_kernel(
@@ -79,351 +72,385 @@ def tile_multiheadlatentattention_pa_kernel(
     nc = tc.nc
     with ExitStack() as ctx:
         keep = ctx.enter_context(tc.tile_pool(name="keep", bufs=1))
-        work = ctx.enter_context(tc.tile_pool(name="work", bufs=3))
-        psum = ctx.enter_context(tc.psum_pool(name="psum", bufs=8))
+        work = ctx.enter_context(tc.tile_pool(name="work", bufs=1))
+        psum = ctx.enter_context(tc.psum_pool(name="psum", bufs=BANKS))
         ctx.enter_context(tc.manual_schedule())
 
-        x_pair = [keep.tile([P, 2, D], BF16, name="x_pair%d" % t, tag="big", bufs=4) for t in range(2)]
-        c_pair = [keep.tile([P, 2, 4, 512], BF16, name="c_pair%d" % t, tag="big", bufs=4) for t in range(2)]
-        qb_raw = [keep.tile([P, 4, 1024], U8, name="qb_raw%d" % g) for g in range(NG)]
-        qd_raw = keep.tile([P, 4, 1024], BF16, name="qd_raw")
-        kd_raw = keep.tile([P, 4, 1024], BF16, name="kd_raw")
-        q_scale = [keep.tile([P, 4], F32, name="q_scale%d" % g) for g in range(NG)]
+        x_raw = [keep.tile([P, 2, D_MODEL], BF16, name="x_raw%d" % i, tag="early", bufs=4) for i in range(2)]
+        c_raw = [keep.tile([P, 2, 4, BANK], BF16, name="c_raw%d" % i, tag="early", bufs=4) for i in range(2)]
+        d_raw = {name: keep.tile([P, 4, WIDTH], BF16, name=name + "_raw") for name in ("qd", "kd")}
+        rq_codes = [keep.tile([P, 4, WIDTH], U8, name="rq_codes%d" % g) for g in range(PASSES)]
+        rq_scale = [keep.tile([P, 4], F32, name="rq_scale%d" % g) for g in range(PASSES)]
         x_rows = x.rearrange("b s d -> (b s) d")
 
+        def pass_rows(src, g):
+            return src[g * PASS : (g + 1) * PASS, :].rearrange("(p t) n -> p t n", t=4)
+
         def load_x(t):
-            nc.sync.dma_start(out=x_pair[t // 2][:, t % 2], in_=x_rows[t * P : (t + 1) * P, :])
+            nc.sync.dma_start(out=x_raw[t // 2][:, t % 2], in_=x_rows[t * P : (t + 1) * P, :])
 
-        def load_w(dst, src, g):
-            nc.sync.dma_start(out=dst, in_=src[g * 512 : (g + 1) * 512, :].rearrange("(p t) n -> p t n", t=4))
+        def load_c_w(g, cols):
+            nc.sync.dma_start(out=c_raw[g // 2][:, g % 2, :, cols], in_=pass_rows(w_c, g)[:, :, cols])
 
-        def load_scale(g):
-            rows = w_rq_scale[g * 512 : (g + 1) * 512, :]
-            nc.scalar.dma_start(out=q_scale[g][:], in_=rows.rearrange("(p t) o -> p (t o)", t=4))
+        def load_rq(g, planes):
+            nc.sync.dma_start(out=rq_codes[g][:, planes, :], in_=pass_rows(w_rq_bytes, g)[:, planes, :])
 
-        load_scale(0)
-        load_w(c_pair[0][:, 0], w_c, 0)
-        load_w(qb_raw[0][:], w_rq_bytes, 0)
-        load_w(c_pair[0][:, 1], w_c, 1)
+        def load_rq_scale(g):
+            nc.sync.dma_start(out=rq_scale[g][:], in_=pass_rows(w_rq_scale, g).rearrange("p t o -> p (t o)"))
+
+        for e in range(2):
+            load_c_w(0, slice(256 * e, 256 * e + 256))
+            if e == 0:
+                load_rq_scale(0)
+            load_rq(0, slice(2 * e, 2 * e + 2))
+        load_rq_scale(1)
+        load_rq(1, slice(0, 4))
         load_x(0)
-        load_x(1)
-        for i in range(2, 4):
-            load_w(c_pair[1][:, i % 2], w_c, i)
+        for i in range(1, PASSES):
+            load_c_w(i, slice(0, BANK))
             load_x(i)
-        load_w(qd_raw[:], w_qd, 0)
-        load_w(qb_raw[1][:], w_rq_bytes, 1)
-        load_w(kd_raw[:], w_kd, 0)
-        load_w(qb_raw[2][:], w_rq_bytes, 2)
+        load_rq_scale(2)
+        nc.sync.dma_start(out=d_raw["qd"][:], in_=pass_rows(w_qd, 0))
+        nc.sync.dma_start(out=d_raw["kd"][:], in_=pass_rows(w_kd, 0))
+        load_rq_scale(3)
+        load_rq(2, slice(0, 4))
 
         zero = keep.tile([P, 1], F32, name="zero")
         nc.gpsimd.memset(zero[:], 0.0)
-        sin_zero = keep.tile([P, 1], F32, name="sin_zero")
-        nc.scalar.activation(out=sin_zero[:], in_=zero[:], func=ACT.Sin)
-        pos = keep.tile([P, TT, 1], F32, name="pos")
+        sin_of_zero = keep.tile([P, 1], F32, name="sin_of_zero")
+        nc.scalar.activation(out=sin_of_zero[:], in_=zero[:], func=ACT.Sin)
+        position = keep.tile([P, TOKEN_TILES, 1], F32, name="position")
         nc.gpsimd.iota(
-            pos[:], pattern=[[P, TT], [0, 1]], base=0, channel_multiplier=1, allow_small_or_imprecise_dtypes=True
+            position[:],
+            pattern=[[P, TOKEN_TILES], [0, 1]],
+            base=0,
+            channel_multiplier=1,
+            allow_small_or_imprecise_dtypes=True,
         )
         ident = keep.tile([P, P], F32, name="ident")
         make_identity(nc, ident[:])
 
-        turns = keep.tile([P, TT, HALF], F32, name="turns")
+        turns_of = keep.tile([P, TOKEN_TILES, HALF], F32, name="turns_of")
         nc.vector.tensor_scalar(
-            out=turns[:, :, 0:1], in0=pos[:], scalar1=1.0 / (2.0 * math.pi), scalar2=None, op0=ALU.mult
+            out=turns_of[:, :, 0:1], in0=position[:], scalar1=1.0 / (2.0 * math.pi), scalar2=None, op0=ALU.mult
         )
         done = 1
         while done < HALF:
             nc.vector.tensor_scalar(
-                out=turns[:, :, done : 2 * done],
-                in0=turns[:, :, 0:done],
-                scalar1=10000.0 ** (-2.0 * done / R),
+                out=turns_of[:, :, done : 2 * done],
+                in0=turns_of[:, :, 0:done],
+                scalar1=10000.0 ** (-2.0 * done / ROTATED),
                 scalar2=None,
                 op0=ALU.mult,
             )
             done *= 2
-        whole = keep.tile([P, TT, HALF], I32, name="whole")
-        nc.vector.tensor_copy(out=whole[:], in_=turns[:])
-        frac = keep.tile([P, TT, HALF], F32, name="frac")
-        nc.vector.tensor_tensor(out=frac[:], in0=turns[:], in1=whole[:], op=ALU.subtract)
-        nfrac = keep.tile([P, TT, HALF], F32, name="nfrac")
+        whole = keep.tile([P, TOKEN_TILES, HALF], I32, name="whole")
+        nc.vector.tensor_copy(out=whole[:], in_=turns_of[:])
+        rest = keep.tile([P, TOKEN_TILES, HALF], F32, name="rest")
+        nc.vector.tensor_tensor(out=rest[:], in0=turns_of[:], in1=whole[:], op=ALU.subtract)
+        minus_rest = keep.tile([P, TOKEN_TILES, HALF], F32, name="minus_rest")
         nc.vector.scalar_tensor_tensor(
-            out=nfrac[:], in0=frac[:], scalar=0.5, in1=frac[:], op0=ALU.is_gt, op1=ALU.subtract
+            out=minus_rest[:], in0=rest[:], scalar=0.5, in1=rest[:], op0=ALU.is_gt, op1=ALU.subtract
         )
-        half_sin = keep.tile([P, TT, HALF], F32, name="half_sin")
-        nc.scalar.activation(out=half_sin[:], in_=nfrac[:], func=ACT.Sin, scale=math.pi)
-        table = keep.tile([P, TT, 2, 2, HALF], F32, name="table")
-        for j, sign in enumerate((-1.0, 1.0)):
-            nc.scalar.activation(out=table[:, :, 1, j, :], in_=nfrac[:], func=ACT.Sin, scale=sign * 2.0 * math.pi)
-        dcos = keep.tile([P, TT, HALF], F32, name="dcos")
+        table = keep.tile([P, TOKEN_TILES, 2, 2, HALF], F32, name="table")
+        half_sin = keep.tile([P, TOKEN_TILES, HALF], F32, name="half_sin")
+        nc.scalar.activation(out=half_sin[:], in_=minus_rest[:], func=ACT.Sin, scale=math.pi)
+        for j, sign in enumerate((1.0, -1.0)):
+            nc.scalar.activation(
+                out=table[:, :, 1, j, :], in_=minus_rest[:], func=ACT.Sin, scale=-sign * 2.0 * math.pi
+            )
+        cos_less_one = keep.tile([P, TOKEN_TILES, HALF], F32, name="cos_less_one")
         nc.vector.scalar_tensor_tensor(
-            out=dcos[:], in0=half_sin[:], scalar=-2.0, in1=half_sin[:], op0=ALU.mult, op1=ALU.mult
+            out=cos_less_one[:], in0=half_sin[:], scalar=-2.0, in1=half_sin[:], op0=ALU.mult, op1=ALU.mult
         )
         for j in range(2):
-            nc.vector.tensor_scalar(out=table[:, :, 0, j, :], in0=dcos[:], scalar1=1.0, scalar2=None, op0=ALU.add)
+            nc.vector.tensor_scalar(
+                out=table[:, :, 0, j, :], in0=cos_less_one[:], scalar1=1.0, scalar2=None, op0=ALU.add
+            )
 
         def operand(name, parts, width):
-            codes = keep.tile([P, parts, width], U32, name=name + "_codes", align_bytes=64)
+            words = keep.tile([P, parts, width], U32, name=name + "_words", align_bytes=64)
             scales = keep.tile([P, parts, width], U8, name=name + "_scales", align_bytes=64)
-            return codes, scales
+            return words, scales
 
-        def quantize(op, part, cols, grouped):
-            nc.vector.quantize_mx(
-                out=op[0][:, part, cols].bitcast(FP8X4), scales=op[1][:, part, cols], in_=grouped
-            )
+        def mx(op, part, cols):
+            return op[0][:, part, cols].bitcast(FP8X4), op[1][:, part, cols]
 
-        x_op = operand("x", TT * NG, P)
-        c_w_op = operand("c_w", NG, 512)
-        c_op = operand("c", TT, P)
-        ops = {
-            "qd": operand("qd", 1, 1024),
-            "kd": operand("kd", 1, 1024),
-            "rq": operand("rq", NG, 1024),
-            "rk": operand("rk", NG, 1024),
-        }
+        def quantize(op, part, cols, turned):
+            words, scales = mx(op, part, cols)
+            nc.vector.quantize_mx(out=words, scales=scales, in_=turned)
 
-        staged = {}
-
-        def x_turn(t):
-            xg = work.tile([P, NG * P * 4], BF16, name="xg", tag="stage", bufs=8, align_bytes=64)
-            words = x_pair[t // 2][:, t % 2].bitcast(F32)
-            xw = xg[:].bitcast(F32).rearrange("p (g r u) -> p g r u", g=NG, u=2)
-            for b in range(2):
-                xt = psum.tile([P, 2, 2, P], F32, name="xt", tag="bank")
-                for e in range(2):
-                    g = 2 * b + e
-                    for u in range(2):
-                        nc.tensor.transpose(
-                            xt[:, e, u, :], words[:, 256 * g + u : 256 * (g + 1) : 2], ident[:]
-                        )
-                nc.scalar.copy(out=xw[:, 2 * b : 2 * b + 2], in_=xt[:].rearrange("p g u r -> p g r u"))
-            staged[("x", t)] = xg
-
-        def x_quant(t):
-            parts = slice(t * NG, (t + 1) * NG)
-            nc.vector.quantize_mx(
-                out=x_op[0][:, parts, :].rearrange("p g n -> p (g n)").bitcast(FP8X4),
-                scales=x_op[1][:, parts, :].rearrange("p g n -> p (g n)"),
-                in_=staged[("x", t)][:],
-            )
-
-        def cw_turn(g):
-            grouped = work.tile([P, 512 * 4], BF16, name="cw_grouped", tag="stage", bufs=8, align_bytes=64)
-            nc.vector.tensor_copy(
-                out=grouped[:].rearrange("p (t m j) -> p t m j", t=4, j=4),
-                in_=c_pair[g // 2][:, g % 2].rearrange("p j (m t) -> p t m j", t=4),
-            )
-            staged[("c_w", g)] = grouped
-
-        def cw_quant(g):
-            quantize(c_w_op, g, slice(0, 512), staged[("c_w", g)][:])
-
-        def c_mm(t):
-            cb = psum.tile([P, 4, P], F32, name="cb", tag="bank")
-            for j in range(4):
-                for g in range(NG):
-                    nc.tensor.matmul_mx(
-                        out=cb[:, j, :],
-                        lhsT=c_w_op[0][:, g, j * P : (j + 1) * P].bitcast(FP8X4),
-                        lhsT_scale=c_w_op[1][:, g, j * P : (j + 1) * P],
-                        rhs=x_op[0][:, t * NG + g, :].bitcast(FP8X4),
-                        rhs_scale=x_op[1][:, t * NG + g, :],
-                        start=(g == 0),
-                        stop=(g == NG - 1),
-                    )
-            cg = work.tile([P, P, 4], BF16, name="cg", bufs=2, align_bytes=64)
-            nc.scalar.copy(out=cg[:], in_=cb[:].rearrange("p t n -> p n t"))
-            staged[("c", t)] = cg
-
-        def c_quant(t):
-            quantize(c_op, t, slice(0, P), staged[("c", t)][:].rearrange("p n t -> p (n t)"))
-
-        def cols_of(half_no):
-            return slice(half_no * 512, half_no * 512 + 512)
-
-        wide_tiles = {}
-        k_raw = {}
-
-        def load_k(g):
-            k_tile = keep.tile([P, 4, 1024], BF16, name="k_raw%d" % g, tag="big", bufs=4)
-            load_w(k_tile[:], w_rk, g)
-            k_raw[g] = k_tile
-
-        def widen_at(s):
-            for g, j, engine in WIDEN.get(s, ()):
-                if g not in wide_tiles:
-                    wide = work.tile([P, 4, 1024], BF16, name="wide", bufs=2, align_bytes=64)
-                    wide_tiles[g] = wide
-                dst = wide_tiles[g][:, j, :]
-                src = qb_raw[g][:, j, :].bitcast(FP8)
-                scale = q_scale[g][:, j : j + 1]
-                if engine == "vector":
-                    nc.vector.tensor_scalar(out=dst, in0=src, scalar1=scale, scalar2=None, op0=ALU.mult)
-                else:
-                    nc.scalar.activation(out=dst, in_=src, func=ACT.Copy, scale=scale)
-
-        def source(unit):
-            kind, half_no, g, v_cols = unit
-            raw = {"qd": qd_raw, "kd": kd_raw, "rq": wide_tiles.get(g), "rk": k_raw.get(g)}[kind]
-            return raw[:, :, cols_of(half_no)]
-
-        def turn(unit):
-            v_cols = unit[3]
-            grouped = work.tile([P, 512, 4], BF16, name="grouped", tag="stage", bufs=8, align_bytes=64)
-            staged[unit] = grouped
-            raw = source(unit)
-            for copy, lo, hi in ((nc.vector.tensor_copy, 0, v_cols), (nc.scalar.copy, v_cols, 512)):
-                if hi > lo:
-                    copy(
-                        out=grouped[:, lo:hi, :].rearrange("p (c i) t -> p c t i", i=4),
-                        in_=raw[:, :, lo:hi].rearrange("p t (c i) -> p c t i", i=4),
-                    )
-
-        def unit_quant(unit):
-            kind, half_no, g, v_cols = unit
-            quantize(ops[kind], g, cols_of(half_no), staged[unit][:].rearrange("p n t -> p (n t)"))
-
-        q_rows = out_q.rearrange("b s h d -> (b s) (h d)").rearrange("(t p) c -> p t c", p=P)
-        k_rows = out_k.rearrange("b s h d -> (b s) (h d)").rearrange("(t p) c -> p t c", p=P)
-        accs = {}
-        prods = {}
-        ress = {}
-
-        def passes_of(kind):
-            return 1 if kind in ("qd", "kd") else NG
-
-        def multiply(kind, half_no, t, g, first, last):
-            if first:
-                acc = psum.tile([P, 512], F32, name="acc", tag="bank")
-                accs[(kind, half_no, t)] = acc
-            moving = ops[kind]
-            fixed, part = (c_op, t) if passes_of(kind) == 1 else (x_op, t * NG + g)
+        def matmul_mx(out, fixed, moving, first, last):
             nc.tensor.matmul_mx(
-                out=accs[(kind, half_no, t)][:],
-                lhsT=fixed[0][:, part, :].bitcast(FP8X4),
-                lhsT_scale=fixed[1][:, part, :],
-                rhs=moving[0][:, g, cols_of(half_no)].bitcast(FP8X4),
-                rhs_scale=moving[1][:, g, cols_of(half_no)],
+                out=out,
+                lhsT=fixed[0],
+                lhsT_scale=fixed[1],
+                rhs=moving[0],
+                rhs_scale=moving[1],
                 start=first,
                 stop=last,
             )
 
-        def multiply_pair(out):
-            kind, half_no, pair = out
-            passes = passes_of(kind)
+        all_tokens = slice(0, P)
+        x_op = operand("x", TOKEN_TILES * PASSES, P)
+        c_w_op = operand("c_w", PASSES, LATENT)
+        c_op = operand("c", TOKEN_TILES, P)
+        weight_op = {
+            "qd": operand("qd", 1, WIDTH),
+            "kd": operand("kd", 1, WIDTH),
+            "rq": operand("rq", PASSES, WIDTH),
+            "rk": operand("rk", PASSES, WIDTH),
+        }
+
+        def staging(name):
+            stage = work.tile([P, 4 * BANK], BF16, name=name, tag="stage", bufs=8, align_bytes=64)
+            return stage
+
+        x_turned = {}
+        c_w_turned = {}
+        c_banks = {}
+        c_turned = {}
+
+        def turn_x(t):
+            stage = staging("x_stage")
+            words = x_raw[t // 2][:, t % 2].bitcast(F32)
+            dst = stage[:].bitcast(F32).rearrange("p (g r u) -> p g r u", g=PASSES, u=2)
+            for b in range(2):
+                bank = psum.tile([P, 2, 2, P], F32, name="x_bank", tag="bank")
+                for e in range(2):
+                    g = 2 * b + e
+                    for u in range(2):
+                        nc.tensor.transpose(bank[:, e, u, :], words[:, 256 * g + u : 256 * (g + 1) : 2], ident[:])
+                nc.scalar.copy(out=dst[:, 2 * b : 2 * b + 2], in_=bank[:].rearrange("p g u r -> p g r u"))
+            x_turned[t] = stage
+
+        def quantize_x(t):
+            parts = slice(t * PASSES, (t + 1) * PASSES)
+            nc.vector.quantize_mx(
+                out=x_op[0][:, parts, :].rearrange("p g r -> p (g r)").bitcast(FP8X4),
+                scales=x_op[1][:, parts, :].rearrange("p g r -> p (g r)"),
+                in_=x_turned[t][:],
+            )
+
+        def turn_c_w(g):
+            stage = staging("c_w_stage")
+            dst = stage[:].rearrange("p (t m j) -> p t m j", t=4, j=4)
+            src = c_raw[g // 2][:, g % 2].rearrange("p j (m t) -> p t m j", t=4)
+            if g % 2 == 0:
+                nc.scalar.copy(out=dst[:, :, 0:64], in_=src[:, :, 0:64])
+                nc.vector.tensor_copy(out=dst[:, :, 64:P], in_=src[:, :, 64:P])
+            else:
+                nc.vector.tensor_copy(out=dst, in_=src)
+            c_w_turned[g] = stage
+
+        def quantize_c_w(g):
+            quantize(c_w_op, g, slice(0, LATENT), c_w_turned[g][:])
+
+        def multiply_c(t):
+            bank = psum.tile([P, 4, P], F32, name="c_bank", tag="bank")
+            for j in range(4):
+                for g in range(PASSES):
+                    matmul_mx(
+                        bank[:, j, :],
+                        mx(c_w_op, g, slice(j * P, (j + 1) * P)),
+                        mx(x_op, t * PASSES + g, all_tokens),
+                        g == 0,
+                        g == PASSES - 1,
+                    )
+            c_banks[t] = bank
+
+        def copy_c(t):
+            stage = work.tile([P, P, 4], BF16, name="c_stage", bufs=4, align_bytes=64)
+            nc.scalar.copy(out=stage[:], in_=c_banks[t][:].rearrange("p j r -> p r j"))
+            c_turned[t] = stage
+
+        def quantize_c(t):
+            quantize(c_op, t, all_tokens, c_turned[t][:].rearrange("p r j -> p (r j)"))
+
+        wide = {}
+        rk_raw = {}
+        weight_turned = {}
+
+        def half_cols(half):
+            return slice(half * BANK, (half + 1) * BANK)
+
+        def load_rk(g):
+            raw = keep.tile([P, 4, WIDTH], BF16, name="rk_raw%d" % g, tag="early", bufs=4)
+            nc.sync.dma_start(out=raw[:], in_=pass_rows(w_rk, g))
+            rk_raw[g] = raw
+
+        def widen(g, j):
+            if g not in wide:
+                planes = work.tile([P, 4, WIDTH], BF16, name="wide", bufs=2, align_bytes=64)
+                wide[g] = planes
+            dst = wide[g][:, j, :]
+            src = rq_codes[g][:, j, :].bitcast(FP8)
+            scale = rq_scale[g][:, j : j + 1]
+            if j in VECTOR_PLANES[g]:
+                nc.vector.tensor_scalar(out=dst, in0=src, scalar1=scale, scalar2=None, op0=ALU.mult)
+            else:
+                nc.scalar.activation(out=dst, in_=src, func=ACT.Copy, scale=scale)
+
+        def turn_unit(unit):
+            name, half, g, vector_cols = unit
+            raw = wide[g] if name == "rq" else rk_raw[g] if name == "rk" else d_raw[name]
+            src = raw[:, :, half_cols(half)]
+            stage = staging("unit_stage")
+            dst = stage[:].rearrange("p (n t) -> p n t", t=4)
+            for copy, lo, hi in ((nc.vector.tensor_copy, 0, vector_cols), (nc.scalar.copy, vector_cols, BANK)):
+                if hi > lo:
+                    copy(
+                        out=dst[:, lo:hi, :].rearrange("p (c i) t -> p c t i", i=4),
+                        in_=src[:, :, lo:hi].rearrange("p t (c i) -> p c t i", i=4),
+                    )
+            weight_turned[unit] = stage
+
+        def quantize_unit(unit):
+            name, half, g, vector_cols = unit
+            quantize(weight_op[name], g, half_cols(half), weight_turned[unit][:])
+
+        q_rows = out_q.rearrange("b s h d -> (b s) (h d)").rearrange("(t p) c -> p t c", p=P)
+        k_rows = out_k.rearrange("b s h d -> (b s) (h d)").rearrange("(t p) c -> p t c", p=P)
+        accs = {}
+        products = {}
+        results = {}
+
+        def from_latent(name):
+            return name in ("qd", "kd")
+
+        def multiply(name, half, t, g, first, last):
+            if first:
+                acc = psum.tile([P, BANK], F32, name="acc", tag="bank")
+                accs[(name, half, t)] = acc
+            fixed = mx(c_op, t, all_tokens) if from_latent(name) else mx(x_op, t * PASSES + g, all_tokens)
+            matmul_mx(accs[(name, half, t)][:], fixed, mx(weight_op[name], g, half_cols(half)), first, last)
+
+        def multiply_group(group):
+            name, half, pair = group
+            passes = 1 if from_latent(name) else PASSES
             for t in (2 * pair, 2 * pair + 1):
                 for g in range(passes):
-                    multiply(kind, half_no, t, g, g == 0, g == passes - 1)
+                    multiply(name, half, t, g, g == 0, g == passes - 1)
 
-        def heads(out, e):
-            kind, half_no, pair = out
-            return accs[(kind, half_no, 2 * pair + e)][:].rearrange("p (h d) -> p h d", h=4)
+        def heads_of(group, e):
+            name, half, pair = group
+            return accs[(name, half, 2 * pair + e)][:].rearrange("p (h d) -> p h d", d=HEAD_DIM)
 
-        def plain(out):
-            res = work.tile([P, 2, 4, DH], F32, name="res", bufs=5)
-            ress[out] = res
+        def copy_plain(group):
+            result = work.tile([P, 2, 4, HEAD_DIM], F32, name="result", bufs=5)
             for e in range(2):
-                nc.scalar.copy(out=res[:, e, :, 0:C], in_=heads(out, e)[:, :, 0:C])
+                nc.scalar.copy(out=result[:, e, :, 0:PLAIN], in_=heads_of(group, e)[:, :, 0:PLAIN])
+            results[group] = result
 
-        def products(out):
-            prod = work.tile([P, 2, 2, 4, R], F32, name="prod", bufs=3)
-            prods[out] = prod
+        def multiply_angles(group):
+            product = work.tile([P, 2, 2, 4, ROTATED], F32, name="product", bufs=3)
             for e in range(2):
+                factors = table[:, 2 * group[2] + e].rearrange("p f j i -> p f (j i)")
                 nc.vector.tensor_tensor(
-                    out=prod[:, :, e],
-                    in0=heads(out, e)[:, :, C:DH].unsqueeze(1).to_broadcast([P, 2, 4, R]),
-                    in1=table[:, 2 * out[2] + e]
-                    .rearrange("p c j i -> p c (j i)")
-                    .unsqueeze(2)
-                    .to_broadcast([P, 2, 4, R]),
+                    out=product[:, :, e],
+                    in0=heads_of(group, e)[:, :, PLAIN:HEAD_DIM].unsqueeze(1).to_broadcast([P, 2, 4, ROTATED]),
+                    in1=factors.unsqueeze(2).to_broadcast([P, 2, 4, ROTATED]),
                     op=ALU.mult,
                 )
+            products[group] = product
 
-        def add_store(out, lo, hi):
-            kind, half_no, pair = out
-            terms = [prods[out][:, c, lo:hi].rearrange("p e h (j i) -> p (e h) j i", j=2) for c in range(2)]
-            nc.vector.tensor_tensor(
-                out=ress[out][:, lo:hi, :, C:DH].rearrange("p e h (j i) -> p (e h) j i", j=2),
-                in0=terms[0],
-                in1=terms[1][:, :, ::-1, :],
+        def add_and_store(engine, group, lo, hi):
+            name, half, pair = group
+            with_cos, with_sin = [
+                products[group][:, f, lo:hi].rearrange("p e h (j i) -> p (e h) j i", j=2) for f in range(2)
+            ]
+            engine.tensor_tensor(
+                out=results[group][:, lo:hi, :, PLAIN:HEAD_DIM].rearrange("p e h (j i) -> p (e h) j i", j=2),
+                in0=with_cos,
+                in1=with_sin[:, :, ::-1, :],
                 op=ALU.add,
             )
-            rows = q_rows if kind in ("qd", "rq") else k_rows
-            col0 = half_no * 512 + (0 if passes_of(kind) == 1 else H * C)
+            rows = q_rows if name in ("qd", "rq") else k_rows
+            col0 = half * BANK + (0 if from_latent(name) else WIDTH)
             nc.sync.dma_start(
-                out=rows[:, 2 * pair + lo : 2 * pair + hi, col0 : col0 + 512],
-                in_=ress[out][:, lo:hi].rearrange("p e h d -> p e (h d)"),
+                out=rows[:, 2 * pair + lo : 2 * pair + hi, col0 : col0 + BANK],
+                in_=results[group][:, lo:hi].rearrange("p e h d -> p e (h d)"),
             )
 
-        for i in range(4):
-            cw_turn(i)
+        for i in range(PASSES):
+            turn_c_w(i)
             if i == 0:
-                widen_at(-5)
+                for g in range(2):
+                    for j in range(4):
+                        widen(g, j)
             else:
-                cw_quant(i - 1)
-                x_quant(i - 1)
-            x_turn(i)
-            widen_at(i - 4)
-        turn(PLAN[0])
-        cw_quant(3)
-        x_quant(3)
-        for g in range(1, NG):
-            load_scale(g)
-        load_k(0)
-        load_k(1)
-        load_w(qb_raw[3][:], w_rq_bytes, 3)
-        load_k(2)
-        load_k(3)
-        c_mm(0)
-        c_mm(1)
-        turn(PLAN[1])
-        c_quant(0)
+                quantize_c_w(i - 1)
+                quantize_x(i - 1)
+            turn_x(i)
+        load_rk(0)
+        load_rk(1)
+        load_rq(3, slice(0, 4))
+        load_rk(2)
+        load_rk(3)
+        turn_unit(UNITS[0])
+        quantize_c_w(PASSES - 1)
+        quantize_x(TOKEN_TILES - 1)
+        for t in range(TOKEN_TILES):
+            multiply_c(t)
+        turn_unit(UNITS[1])
 
-        n = len(PLAN)
-        final = PLAN[n - 4 :]
-        banks = 0
-        ready = set()
+        steps = len(UNITS)
+        last_units = UNITS[steps - PASSES :]
+        group_at = {}
+        for name, at in OUTPUT_STEPS.items():
+            for i, s in enumerate(at):
+                group_at[s] = (name, i // 2, i % 2)
+        last_group = max(group_at)
+        banks_used = TOKEN_TILES
+        quantised = set()
+        latent_tiles = set()
         multiplied = set()
-        last_step = max(OUTS)
-        for s in range(last_step + 3):
-            if s < n:
-                unit_quant(PLAN[s])
-                ready.add(PLAN[s][:3])
-            if s == 0:
-                c_mm(2)
-                c_quant(1)
-                c_mm(3)
-            if s == 1:
-                c_quant(2)
-            if s + 2 < n:
-                turn(PLAN[s + 2])
-            if s == 1:
-                c_quant(3)
-            if s - 1 in OUTS:
-                products(OUTS[s - 1])
-                banks -= 2
-            if s - 2 in OUTS:
-                if s - 2 == last_step:
-                    add_store(OUTS[s - 2], 0, 1)
-                    add_store(OUTS[s - 2], 1, 2)
+        for s in range(last_group + 3):
+            if s < steps:
+                quantize_unit(UNITS[s])
+                quantised.add(UNITS[s][:3])
+            if s + 2 < steps:
+                turn_unit(UNITS[s + 2])
+            if s < TOKEN_TILES:
+                copy_c(s)
+                banks_used -= 1
+            if 1 <= s <= TOKEN_TILES:
+                quantize_c(s - 1)
+                latent_tiles.add(s - 1)
+            if s - 1 in group_at:
+                multiply_angles(group_at[s - 1])
+                banks_used -= 2
+            if s - 2 in group_at:
+                if s - 2 == last_group:
+                    add_and_store(nc.vector, group_at[s - 2], 0, 1)
+                    add_and_store(nc.vector, group_at[s - 2], 1, 2)
                 else:
-                    add_store(OUTS[s - 2], 0, 2)
-            if s in OUTS:
-                plain(OUTS[s])
-            if s == n - 2:
-                banks += 4
-                for unit in final[:3]:
-                    for t in range(TT):
-                        multiply(unit[0], unit[1], t, unit[2], unit == final[0], False)
-            if s == n - 1:
-                for t in range(TT):
-                    multiply(final[3][0], final[3][1], t, final[3][2], False, True)
-            for out in (OUTS.get(s + 1), OUTS.get(s + 2)):
-                if out is not None and out[:2] != final[0][:2] and out not in multiplied:
-                    kind, half_no, pair = out
-                    if banks + 2 > 8 or any((kind, half_no, g) not in ready for g in range(passes_of(kind))):
-                        break
-                    if passes_of(kind) == 1 and s < pair:
-                        break
-                    multiply_pair(out)
-                    multiplied.add(out)
-                    banks += 2
-            widen_at(s)
+                    engine = nc.gpsimd if s >= steps else nc.vector
+                    add_and_store(engine, group_at[s - 2], 0, 2)
+            if s in group_at:
+                copy_plain(group_at[s])
+            if s == steps - 2:
+                banks_used += TOKEN_TILES
+                for name, half, g, vector_cols in last_units[:-1]:
+                    for t in range(TOKEN_TILES):
+                        multiply(name, half, t, g, g == 0, False)
+            if s == steps - 1:
+                name, half, g, vector_cols = last_units[-1]
+                for t in range(TOKEN_TILES):
+                    multiply(name, half, t, g, False, True)
+            for ahead in (s + 1, s + 2):
+                group = group_at.get(ahead)
+                if group is None or group in multiplied or group[:2] == last_units[0][:2]:
+                    continue
+                name, half, pair = group
+                if from_latent(name):
+                    ready = (name, half, 0) in quantised and {2 * pair, 2 * pair + 1} <= latent_tiles
+                else:
+                    ready = all((name, half, g) in quantised for g in range(PASSES))
+                if not ready or banks_used + 2 > BANKS:
+                    break
+                multiply_group(group)
+                multiplied.add(group)
+                banks_used += 2
+            for g, j in WIDEN_STEPS.get(s, ()):
+                widen(g, j)

import math
from contextlib import ExitStack

import concourse.mybir as mybir
from concourse.masks import make_identity

F32 = mybir.dt.float32
BF16 = mybir.dt.bfloat16
I32 = mybir.dt.int32
U32 = mybir.dt.uint32
U8 = mybir.dt.uint8
FP8 = mybir.dt.float8_e4m3fn
FP8X4 = mybir.dt.float8_e4m3fn_x4
ALU = mybir.AluOpType
ACT = mybir.ActivationFunctionType

P = 128
TOKENS, D_MODEL, HEADS, HEAD_DIM, LATENT, ROTATED = 512, 2048, 16, 128, 512, 64
PLAIN = HEAD_DIM - ROTATED
HALF = ROTATED // 2
PASS = 512
PASSES = D_MODEL // PASS
TOKEN_TILES = TOKENS // P
BANK = 512
BANKS = 8
WIDTH = 2 * BANK
FLOPS = 2 * TOKENS * (D_MODEL * LATENT + 2 * LATENT * WIDTH + 2 * D_MODEL * WIDTH)

UNITS = (
    ("qd", 0, 0, 0),
    ("qd", 1, 0, 512),
    ("kd", 0, 0, 128),
    ("kd", 1, 0, 384),
    ("rq", 0, 0, 512),
    ("rq", 0, 1, 0),
    ("rq", 1, 0, 512),
    ("rq", 1, 1, 0),
    ("rk", 0, 0, 0),
    ("rk", 0, 1, 512),
    ("rk", 0, 2, 384),
    ("rk", 0, 3, 512),
    ("rq", 0, 2, 0),
    ("rq", 0, 3, 512),
    ("rq", 1, 2, 0),
    ("rq", 1, 3, 0),
    ("rk", 1, 0, 0),
    ("rk", 1, 1, 256),
    ("rk", 1, 2, 0),
    ("rk", 1, 3, 0),
)

OUTPUT_STEPS = {
    "qd": (3, 5, 6, 7),
    "kd": (8, 10, 11, 14),
    "rk": (12, 13, 20, 21),
    "rq": (16, 18, 19, 22),
}

WIDEN_STEPS = {
    4: ((3, 3),),
    6: ((2, 0),),
    7: ((2, 1), (2, 2)),
    8: ((2, 3), (3, 0), (3, 1)),
    9: ((3, 2),),
}
VECTOR_PLANES = ((3,), (1, 2, 3), (), (3,))


def tile_multiheadlatentattention_pa_kernel(
    tc, x, w_c, w_qd, w_kd, w_rq_bytes, w_rq_scale, w_rk, out_q, out_k
):
    nc = tc.nc
    with ExitStack() as ctx:
        keep = ctx.enter_context(tc.tile_pool(name="keep", bufs=1))
        work = ctx.enter_context(tc.tile_pool(name="work", bufs=1))
        psum = ctx.enter_context(tc.psum_pool(name="psum", bufs=BANKS))
        ctx.enter_context(tc.manual_schedule())

        x_raw = [keep.tile([P, 2, D_MODEL], BF16, name="x_raw%d" % i, tag="early", bufs=4) for i in range(2)]
        c_raw = [keep.tile([P, 2, 4, BANK], BF16, name="c_raw%d" % i, tag="early", bufs=4) for i in range(2)]
        d_raw = {name: keep.tile([P, 4, WIDTH], BF16, name=name + "_raw") for name in ("qd", "kd")}
        rq_codes = [keep.tile([P, 4, WIDTH], U8, name="rq_codes%d" % g) for g in range(PASSES)]
        rq_scale = [keep.tile([P, 4], F32, name="rq_scale%d" % g) for g in range(PASSES)]
        x_rows = x.rearrange("b s d -> (b s) d")

        def pass_rows(src, g):
            return src[g * PASS : (g + 1) * PASS, :].rearrange("(p t) n -> p t n", t=4)

        def load_x(t):
            nc.sync.dma_start(out=x_raw[t // 2][:, t % 2], in_=x_rows[t * P : (t + 1) * P, :])

        def load_c_w(g, cols):
            nc.sync.dma_start(out=c_raw[g // 2][:, g % 2, :, cols], in_=pass_rows(w_c, g)[:, :, cols])

        def load_rq(g, planes):
            nc.sync.dma_start(out=rq_codes[g][:, planes, :], in_=pass_rows(w_rq_bytes, g)[:, planes, :])

        def load_rq_scale(g):
            nc.sync.dma_start(out=rq_scale[g][:], in_=pass_rows(w_rq_scale, g).rearrange("p t o -> p (t o)"))

        for e in range(2):
            load_c_w(0, slice(256 * e, 256 * e + 256))
            if e == 0:
                load_rq_scale(0)
            load_rq(0, slice(2 * e, 2 * e + 2))
        load_rq_scale(1)
        load_rq(1, slice(0, 4))
        load_x(0)
        for i in range(1, PASSES):
            load_c_w(i, slice(0, BANK))
            load_x(i)
        load_rq_scale(2)
        nc.sync.dma_start(out=d_raw["qd"][:], in_=pass_rows(w_qd, 0))
        nc.sync.dma_start(out=d_raw["kd"][:], in_=pass_rows(w_kd, 0))
        load_rq_scale(3)
        load_rq(2, slice(0, 4))

        zero = keep.tile([P, 1], F32, name="zero")
        nc.gpsimd.memset(zero[:], 0.0)
        sin_of_zero = keep.tile([P, 1], F32, name="sin_of_zero")
        nc.scalar.activation(out=sin_of_zero[:], in_=zero[:], func=ACT.Sin)
        position = keep.tile([P, TOKEN_TILES, 1], F32, name="position")
        nc.gpsimd.iota(
            position[:],
            pattern=[[P, TOKEN_TILES], [0, 1]],
            base=0,
            channel_multiplier=1,
            allow_small_or_imprecise_dtypes=True,
        )
        ident = keep.tile([P, P], F32, name="ident")
        make_identity(nc, ident[:])

        turns_of = keep.tile([P, TOKEN_TILES, HALF], F32, name="turns_of")
        nc.vector.tensor_scalar(
            out=turns_of[:, :, 0:1], in0=position[:], scalar1=1.0 / (2.0 * math.pi), scalar2=None, op0=ALU.mult
        )
        done = 1
        while done < HALF:
            nc.vector.tensor_scalar(
                out=turns_of[:, :, done : 2 * done],
                in0=turns_of[:, :, 0:done],
                scalar1=10000.0 ** (-2.0 * done / ROTATED),
                scalar2=None,
                op0=ALU.mult,
            )
            done *= 2
        whole = keep.tile([P, TOKEN_TILES, HALF], I32, name="whole")
        nc.vector.tensor_copy(out=whole[:], in_=turns_of[:])
        rest = keep.tile([P, TOKEN_TILES, HALF], F32, name="rest")
        nc.vector.tensor_tensor(out=rest[:], in0=turns_of[:], in1=whole[:], op=ALU.subtract)
        minus_rest = keep.tile([P, TOKEN_TILES, HALF], F32, name="minus_rest")
        nc.vector.scalar_tensor_tensor(
            out=minus_rest[:], in0=rest[:], scalar=0.5, in1=rest[:], op0=ALU.is_gt, op1=ALU.subtract
        )
        table = keep.tile([P, TOKEN_TILES, 2, 2, HALF], F32, name="table")
        half_sin = keep.tile([P, TOKEN_TILES, HALF], F32, name="half_sin")
        nc.scalar.activation(out=half_sin[:], in_=minus_rest[:], func=ACT.Sin, scale=math.pi)
        for j, sign in enumerate((1.0, -1.0)):
            nc.scalar.activation(
                out=table[:, :, 1, j, :], in_=minus_rest[:], func=ACT.Sin, scale=-sign * 2.0 * math.pi
            )
        cos_less_one = keep.tile([P, TOKEN_TILES, HALF], F32, name="cos_less_one")
        nc.vector.scalar_tensor_tensor(
            out=cos_less_one[:], in0=half_sin[:], scalar=-2.0, in1=half_sin[:], op0=ALU.mult, op1=ALU.mult
        )
        for j in range(2):
            nc.vector.tensor_scalar(
                out=table[:, :, 0, j, :], in0=cos_less_one[:], scalar1=1.0, scalar2=None, op0=ALU.add
            )

        def operand(name, parts, width):
            words = keep.tile([P, parts, width], U32, name=name + "_words", align_bytes=64)
            scales = keep.tile([P, parts, width], U8, name=name + "_scales", align_bytes=64)
            return words, scales

        def mx(op, part, cols):
            return op[0][:, part, cols].bitcast(FP8X4), op[1][:, part, cols]

        def quantize(op, part, cols, turned):
            words, scales = mx(op, part, cols)
            nc.vector.quantize_mx(out=words, scales=scales, in_=turned)

        def matmul_mx(out, fixed, moving, first, last):
            nc.tensor.matmul_mx(
                out=out,
                lhsT=fixed[0],
                lhsT_scale=fixed[1],
                rhs=moving[0],
                rhs_scale=moving[1],
                start=first,
                stop=last,
            )

        all_tokens = slice(0, P)
        x_op = operand("x", TOKEN_TILES * PASSES, P)
        c_w_op = operand("c_w", PASSES, LATENT)
        c_op = operand("c", TOKEN_TILES, P)
        weight_op = {
            "qd": operand("qd", 1, WIDTH),
            "kd": operand("kd", 1, WIDTH),
            "rq": operand("rq", PASSES, WIDTH),
            "rk": operand("rk", PASSES, WIDTH),
        }

        def staging(name):
            stage = work.tile([P, 4 * BANK], BF16, name=name, tag="stage", bufs=8, align_bytes=64)
            return stage

        x_turned = {}
        c_w_turned = {}
        c_banks = {}
        c_turned = {}

        def turn_x(t):
            stage = staging("x_stage")
            words = x_raw[t // 2][:, t % 2].bitcast(F32)
            dst = stage[:].bitcast(F32).rearrange("p (g r u) -> p g r u", g=PASSES, u=2)
            for b in range(2):
                bank = psum.tile([P, 2, 2, P], F32, name="x_bank", tag="bank")
                for e in range(2):
                    g = 2 * b + e
                    for u in range(2):
                        nc.tensor.transpose(bank[:, e, u, :], words[:, 256 * g + u : 256 * (g + 1) : 2], ident[:])
                nc.scalar.copy(out=dst[:, 2 * b : 2 * b + 2], in_=bank[:].rearrange("p g u r -> p g r u"))
            x_turned[t] = stage

        def quantize_x(t):
            parts = slice(t * PASSES, (t + 1) * PASSES)
            nc.vector.quantize_mx(
                out=x_op[0][:, parts, :].rearrange("p g r -> p (g r)").bitcast(FP8X4),
                scales=x_op[1][:, parts, :].rearrange("p g r -> p (g r)"),
                in_=x_turned[t][:],
            )

        def turn_c_w(g):
            stage = staging("c_w_stage")
            dst = stage[:].rearrange("p (t m j) -> p t m j", t=4, j=4)
            src = c_raw[g // 2][:, g % 2].rearrange("p j (m t) -> p t m j", t=4)
            if g % 2 == 0:
                nc.scalar.copy(out=dst[:, :, 0:64], in_=src[:, :, 0:64])
                nc.vector.tensor_copy(out=dst[:, :, 64:P], in_=src[:, :, 64:P])
            else:
                nc.vector.tensor_copy(out=dst, in_=src)
            c_w_turned[g] = stage

        def quantize_c_w(g):
            quantize(c_w_op, g, slice(0, LATENT), c_w_turned[g][:])

        def multiply_c(t):
            bank = psum.tile([P, 4, P], F32, name="c_bank", tag="bank")
            for j in range(4):
                for g in range(PASSES):
                    matmul_mx(
                        bank[:, j, :],
                        mx(c_w_op, g, slice(j * P, (j + 1) * P)),
                        mx(x_op, t * PASSES + g, all_tokens),
                        g == 0,
                        g == PASSES - 1,
                    )
            c_banks[t] = bank

        def copy_c(t):
            stage = work.tile([P, P, 4], BF16, name="c_stage", bufs=4, align_bytes=64)
            nc.scalar.copy(out=stage[:], in_=c_banks[t][:].rearrange("p j r -> p r j"))
            c_turned[t] = stage

        def quantize_c(t):
            quantize(c_op, t, all_tokens, c_turned[t][:].rearrange("p r j -> p (r j)"))

        wide = {}
        rk_raw = {}
        weight_turned = {}

        def half_cols(half):
            return slice(half * BANK, (half + 1) * BANK)

        def load_rk(g):
            raw = keep.tile([P, 4, WIDTH], BF16, name="rk_raw%d" % g, tag="early", bufs=4)
            nc.sync.dma_start(out=raw[:], in_=pass_rows(w_rk, g))
            rk_raw[g] = raw

        def widen(g, j):
            if g not in wide:
                planes = work.tile([P, 4, WIDTH], BF16, name="wide", bufs=2, align_bytes=64)
                wide[g] = planes
            dst = wide[g][:, j, :]
            src = rq_codes[g][:, j, :].bitcast(FP8)
            scale = rq_scale[g][:, j : j + 1]
            if j in VECTOR_PLANES[g]:
                nc.vector.tensor_scalar(out=dst, in0=src, scalar1=scale, scalar2=None, op0=ALU.mult)
            else:
                nc.scalar.activation(out=dst, in_=src, func=ACT.Copy, scale=scale)

        def turn_unit(unit):
            name, half, g, vector_cols = unit
            raw = wide[g] if name == "rq" else rk_raw[g] if name == "rk" else d_raw[name]
            src = raw[:, :, half_cols(half)]
            stage = staging("unit_stage")
            dst = stage[:].rearrange("p (n t) -> p n t", t=4)
            for copy, lo, hi in ((nc.vector.tensor_copy, 0, vector_cols), (nc.scalar.copy, vector_cols, BANK)):
                if hi > lo:
                    copy(
                        out=dst[:, lo:hi, :].rearrange("p (c i) t -> p c t i", i=4),
                        in_=src[:, :, lo:hi].rearrange("p t (c i) -> p c t i", i=4),
                    )
            weight_turned[unit] = stage

        def quantize_unit(unit):
            name, half, g, vector_cols = unit
            quantize(weight_op[name], g, half_cols(half), weight_turned[unit][:])

        q_rows = out_q.rearrange("b s h d -> (b s) (h d)").rearrange("(t p) c -> p t c", p=P)
        k_rows = out_k.rearrange("b s h d -> (b s) (h d)").rearrange("(t p) c -> p t c", p=P)
        accs = {}
        products = {}
        results = {}

        def from_latent(name):
            return name in ("qd", "kd")

        def multiply(name, half, t, g, first, last):
            if first:
                acc = psum.tile([P, BANK], F32, name="acc", tag="bank")
                accs[(name, half, t)] = acc
            fixed = mx(c_op, t, all_tokens) if from_latent(name) else mx(x_op, t * PASSES + g, all_tokens)
            matmul_mx(accs[(name, half, t)][:], fixed, mx(weight_op[name], g, half_cols(half)), first, last)

        def multiply_group(group):
            name, half, pair = group
            passes = 1 if from_latent(name) else PASSES
            for t in (2 * pair, 2 * pair + 1):
                for g in range(passes):
                    multiply(name, half, t, g, g == 0, g == passes - 1)

        def heads_of(group, e):
            name, half, pair = group
            return accs[(name, half, 2 * pair + e)][:].rearrange("p (h d) -> p h d", d=HEAD_DIM)

        def copy_plain(group):
            result = work.tile([P, 2, 4, HEAD_DIM], F32, name="result", bufs=5)
            for e in range(2):
                nc.scalar.copy(out=result[:, e, :, 0:PLAIN], in_=heads_of(group, e)[:, :, 0:PLAIN])
            results[group] = result

        def multiply_angles(group):
            product = work.tile([P, 2, 2, 4, ROTATED], F32, name="product", bufs=3)
            for e in range(2):
                factors = table[:, 2 * group[2] + e].rearrange("p f j i -> p f (j i)")
                nc.vector.tensor_tensor(
                    out=product[:, :, e],
                    in0=heads_of(group, e)[:, :, PLAIN:HEAD_DIM].unsqueeze(1).to_broadcast([P, 2, 4, ROTATED]),
                    in1=factors.unsqueeze(2).to_broadcast([P, 2, 4, ROTATED]),
                    op=ALU.mult,
                )
            products[group] = product

        def add_and_store(engine, group, lo, hi):
            name, half, pair = group
            with_cos, with_sin = [
                products[group][:, f, lo:hi].rearrange("p e h (j i) -> p (e h) j i", j=2) for f in range(2)
            ]
            engine.tensor_tensor(
                out=results[group][:, lo:hi, :, PLAIN:HEAD_DIM].rearrange("p e h (j i) -> p (e h) j i", j=2),
                in0=with_cos,
                in1=with_sin[:, :, ::-1, :],
                op=ALU.add,
            )
            rows = q_rows if name in ("qd", "rq") else k_rows
            col0 = half * BANK + (0 if from_latent(name) else WIDTH)
            nc.sync.dma_start(
                out=rows[:, 2 * pair + lo : 2 * pair + hi, col0 : col0 + BANK],
                in_=results[group][:, lo:hi].rearrange("p e h d -> p e (h d)"),
            )

        for i in range(PASSES):
            turn_c_w(i)
            if i == 0:
                for g in range(2):
                    for j in range(4):
                        widen(g, j)
            else:
                quantize_c_w(i - 1)
                quantize_x(i - 1)
            turn_x(i)
        load_rk(0)
        load_rk(1)
        load_rq(3, slice(0, 4))
        load_rk(2)
        load_rk(3)
        turn_unit(UNITS[0])
        quantize_c_w(PASSES - 1)
        quantize_x(TOKEN_TILES - 1)
        for t in range(TOKEN_TILES):
            multiply_c(t)
        turn_unit(UNITS[1])

        steps = len(UNITS)
        last_units = UNITS[steps - PASSES :]
        group_at = {}
        for name, at in OUTPUT_STEPS.items():
            for i, s in enumerate(at):
                group_at[s] = (name, i // 2, i % 2)
        last_group = max(group_at)
        banks_used = TOKEN_TILES
        quantised = set()
        latent_tiles = set()
        multiplied = set()
        for s in range(last_group + 3):
            if s < steps:
                quantize_unit(UNITS[s])
                quantised.add(UNITS[s][:3])
            if s + 2 < steps:
                turn_unit(UNITS[s + 2])
            if s < TOKEN_TILES:
                copy_c(s)
                banks_used -= 1
            if 1 <= s <= TOKEN_TILES:
                quantize_c(s - 1)
                latent_tiles.add(s - 1)
            if s - 1 in group_at:
                multiply_angles(group_at[s - 1])
                banks_used -= 2
            if s - 2 in group_at:
                if s - 2 == last_group:
                    add_and_store(nc.vector, group_at[s - 2], 0, 1)
                    add_and_store(nc.vector, group_at[s - 2], 1, 2)
                else:
                    engine = nc.gpsimd if s >= steps else nc.vector
                    add_and_store(engine, group_at[s - 2], 0, 2)
            if s in group_at:
                copy_plain(group_at[s])
            if s == steps - 2:
                banks_used += TOKEN_TILES
                for name, half, g, vector_cols in last_units[:-1]:
                    for t in range(TOKEN_TILES):
                        multiply(name, half, t, g, g == 0, False)
            if s == steps - 1:
                name, half, g, vector_cols = last_units[-1]
                for t in range(TOKEN_TILES):
                    multiply(name, half, t, g, False, True)
            for ahead in (s + 1, s + 2):
                group = group_at.get(ahead)
                if group is None or group in multiplied or group[:2] == last_units[0][:2]:
                    continue
                name, half, pair = group
                if from_latent(name):
                    ready = (name, half, 0) in quantised and {2 * pair, 2 * pair + 1} <= latent_tiles
                else:
                    ready = all((name, half, g) in quantised for g in range(PASSES))
                if not ready or banks_used + 2 > BANKS:
                    break
                multiply_group(group)
                multiplied.add(group)
                banks_used += 2
            for g, j in WIDEN_STEPS.get(s, ()):
                widen(g, j)
